import numpy as np
import ml_dtypes


def mxq(x, axis, fmt="e4m3"):
    dtype, down = {"e4m3": (ml_dtypes.float8_e4m3fn, 7), "e5m2": (ml_dtypes.float8_e5m2, 14)}[fmt]
    v = np.moveaxis(np.asarray(x, np.float32).astype(ml_dtypes.bfloat16).astype(np.float64), axis, -1)
    blocks = v.reshape(v.shape[:-1] + (-1, 32))
    amax = np.abs(blocks).max(-1, keepdims=True)
    byte = np.maximum(np.where(amax > 0, np.frexp(amax)[1] - 1 + 127, 0) - down, 1)
    scale = np.exp2(byte - 127.0)
    codes = (blocks / scale).astype(np.float32).astype(dtype).astype(np.float64)
    return np.moveaxis((codes * scale).reshape(v.shape), -1, axis)


WIDE = False


def mx_kscale(k):
    if not WIDE:
        return np.ones(k)
    levels = np.array([10, -10, 5, -5, 0])
    if k % 512:
        return np.exp2(np.random.permutation(np.resize(levels, k // 32))).repeat(32)
    a = np.empty((k // 512, 16))
    for p in range(k // 512):
        a[p, :8] = np.random.permutation(np.resize(levels, 8))
        for g in range(8):
            far = levels[np.abs(levels - a[p, g]) >= 10]
            a[p, g + 8] = far[np.random.randint(len(far))]
    return np.exp2(a.ravel()).repeat(32)


BF16 = ml_dtypes.bfloat16


def bf(x):
    return np.asarray(x, np.float32).astype(BF16)


def f64(x):
    return np.asarray(x).astype(np.float64)


B, S, E, H, KV, HD, HID = 2, 2048, 512, 4, 2, 128, 3072
F = (H + 2 * KV) * HD
EPS = 1e-6
ROPE_BASE = 1000000.0


def rmsnorm(v, w):
    var = np.mean(v * v, axis=-1, keepdims=True)
    return v * (1.0 / np.sqrt(var + EPS)) * w


def apply_rope(v, cos, sin):
    v1 = v[..., 0::2]
    v2 = v[..., 1::2]
    r1 = v1 * cos - v2 * sin
    r2 = v1 * sin + v2 * cos
    return np.stack([r1, r2], axis=-1).reshape(v.shape)


def setup_inputs():
    s = mx_kscale(E)
    return {"x": bf(np.random.standard_normal((B, S, E)) * 2.0),
            "ln_w": bf((1.0 + 0.1 * np.random.standard_normal(E)) * s),
            "qkv_w": bf(np.random.standard_normal((E, F)) * 2.0 / np.sqrt(E) / s[:, None]),
            "q_norm_w": bf(1.0 + 0.1 * np.random.standard_normal(HD)),
            "k_norm_w": bf(1.0 + 0.1 * np.random.standard_normal(HD))}


def reference(x, ln_w, qkv_w, q_norm_w, k_norm_w):
    h = rmsnorm(f64(x), f64(ln_w))
    qkv = mxq(h, 2, "e4m3") @ mxq(f64(qkv_w), 0, "e4m3")
    q = qkv[..., : H * HD].reshape(B, S, H, HD)
    k = qkv[..., H * HD : (H + KV) * HD].reshape(B, S, KV, HD)
    v = qkv[..., (H + KV) * HD :].reshape(B, S, KV, HD)
    q = rmsnorm(q, f64(q_norm_w))
    k = rmsnorm(k, f64(k_norm_w))
    pos = np.arange(S, dtype=np.float64)
    inv_freq = 1.0 / (ROPE_BASE ** (np.arange(0, HD, 2, dtype=np.float64) / HD))
    ang = pos[:, None] * inv_freq
    cos = np.cos(ang)[None, :, None, :]
    sin = np.sin(ang)[None, :, None, :]
    return apply_rope(q, cos, sin), apply_rope(k, cos, sin), v

@@ -1,0 +1,360 @@
+import math
+from contextlib import ExitStack
+
+import concourse.mybir as mybir
+from concourse.masks import make_identity
+
+FLOPS = 2 * 4096 * 512 * 1024
+
+F32 = mybir.dt.float32
+BF16 = mybir.dt.bfloat16
+I32 = mybir.dt.int32
+U32 = mybir.dt.uint32
+U8 = mybir.dt.uint8
+FP8X4 = mybir.dt.float8_e4m3fn_x4
+ALU = mybir.AluOpType
+ACT = mybir.ActivationFunctionType
+
+P = 128
+PACK = 4
+E = P * PACK
+A = 16
+NT = 2 * A
+HD = 128
+PAIRS = HD // 2
+NQ = 4
+NH = 6
+QK = NH * HD
+F = 1024
+BANK = 512
+EPS = 1e-6
+ROPE_BASE = 1000000.0
+
+QUANT_BATCH = (1, 1, 2, 4, 4, 4, 4, 4, 4, 4)
+EARLY = 4
+LAG_RSQRT = 1
+LAG_SCALE = 2
+LAG_TRANSPOSE = 4
+LAG_ROUND = 5
+LAG_QUANT = 6
+LAG_MATMUL = 1
+LAG_HEADNORM = 2
+LAG_ROTATE = 3
+LAG_SUM = 4
+LEAD = LAG_QUANT + max(QUANT_BATCH)
+TABLES_AT_START = 4
+
+
+def quant_batches():
+    first, table = 0, {}
+    for qb, nb in enumerate(QUANT_BATCH):
+        for i in range(first, first + nb):
+            table[i] = (qb, first, nb)
+        first += nb
+    assert first == NT
+    return table
+
+
+def slots_by_step(step):
+    return min(LAG_QUANT + 1 + 2 * step, step + LEAD)
+
+
+def tile_qwen3block_pa_t_kernel(tc, x, ln_w, qkv_w, q_norm_w, k_norm_w, out_0, out_1, out_2):
+    nc = tc.nc
+    with ExitStack() as ctx:
+        const = ctx.enter_context(tc.tile_pool(name="const", bufs=1))
+        small = ctx.enter_context(tc.tile_pool(name="small", bufs=4))
+        xs_pool = ctx.enter_context(tc.tile_pool(name="xs_pool", bufs=4))
+        h_pool = ctx.enter_context(tc.tile_pool(name="h_pool", bufs=3))
+        c_pool = ctx.enter_context(tc.tile_pool(name="c_pool", bufs=3))
+        j_pool = ctx.enter_context(tc.tile_pool(name="j_pool", bufs=3))
+        t_pool = ctx.enter_context(tc.tile_pool(name="t_pool", bufs=3))
+        o_pool = ctx.enter_context(tc.tile_pool(name="o_pool", bufs=4))
+        ps_t = ctx.enter_context(tc.psum_pool(name="ps_t", bufs=2))
+        ps_mx = ctx.enter_context(tc.psum_pool(name="ps_mx", bufs=3))
+        ctx.enter_context(tc.manual_schedule())
+
+        xv = x.rearrange("b (p a) e -> b p a e", a=A)
+        o0v = out_0.rearrange("b (p a) h d -> b p a (h d)", a=A)
+        o1v = out_1.rearrange("b (p a) h d -> b p a (h d)", a=A)
+        o2v = out_2.rearrange("b (p a) h d -> b p a (h d)", a=A)
+
+        def tile_coords(i):
+            g = i // 2
+            return g // 2, g % 2, i % 2
+
+        lnw_b = const.tile([P, PACK], BF16)
+        nc.scalar.dma_start(out=lnw_b[:], in_=ln_w.rearrange("(p t) -> p t", t=PACK))
+
+        xin = {}
+        wr = const.tile([P, PACK, F], BF16)
+        wn = const.tile([P, 2, HD], BF16)
+        for g in range(NT // 2):
+            ap, b = g // 2, g % 2
+            xg = const.tile([P, 2, E], BF16, name="xg%d" % g)
+            nc.sync.dma_start(out=xg[:], in_=xv[b, :, 2 * ap : 2 * ap + 2, :])
+            xin[g] = xg
+            if g == 1:
+                nc.sync.dma_start(out=wr[:], in_=qkv_w.rearrange("(p t) n -> p t n", t=PACK))
+                nc.sync.dma_start(out=wn[:, 0, :], in_=q_norm_w.partition_broadcast(P))
+                nc.sync.dma_start(out=wn[:, 1, :], in_=k_norm_w.partition_broadcast(P))
+
+        ssx = const.tile([P, NT], F32)
+        rx = const.tile([P, NT], F32)
+        eps_t = const.tile([P, 1], F32)
+        nc.vector.memset(eps_t[:], EPS)
+        st = {}
+        batches = quant_batches()
+
+        def stage_square(i):
+            xt = xin[i // 2][:, i % 2, :]
+            junk_x = j_pool.tile([P, E], BF16)
+            nc.scalar.activation(out=junk_x[:], in_=xt, func=ACT.Square, accum_out=ssx[:, i : i + 1])
+
+        def stage_rsqrt(i, n=1):
+            nc.scalar.activation(
+                out=rx[:, i : i + n], in_=ssx[:, i : i + n], func=ACT.Abs_reciprocal_sqrt,
+                scale=1.0 / E, bias=eps_t[:],
+            )
+
+        pos_i = const.tile([P, A], I32)
+        nc.gpsimd.iota(pos_i[:], pattern=[[1, A]], base=0, channel_multiplier=A)
+        identf = const.tile([P, P], F32)
+        make_identity(nc, identf[:])
+
+        one1 = const.tile([P, 1], F32)
+        nc.vector.memset(one1[:], 1.0)
+        gt = const.tile([P, PAIRS], F32)
+        for j in range(4):
+            nc.vector.tensor_scalar_mul(
+                out=gt[:, j : j + 1], in0=one1[:], scalar1=ROPE_BASE ** (-j / 64.0) / (2.0 * math.pi)
+            )
+        for width in (4, 16):
+            for m in range(1, 4):
+                nc.vector.tensor_scalar_mul(
+                    out=gt[:, width * m : width * m + width], in0=gt[:, 0:width],
+                    scalar1=ROPE_BASE ** (-width * m / 64.0),
+                )
+        pos_f = const.tile([P, A], F32)
+        nc.vector.tensor_copy(out=pos_f[:], in_=pos_i[:])
+
+        for i in range(EARLY):
+            stage_square(i)
+
+        tt = const.tile([P, A, PAIRS], F32)
+        n_s = const.tile([P, A, PAIRS], I32)
+        n_c = const.tile([P, A, PAIRS], I32)
+        fr = const.tile([P, 3, A, PAIRS], F32)
+        trig = const.tile([P, A, 2 * HD], F32)
+        for a0, a1 in ((0, A // 2), (A // 2, A)):
+            na = a1 - a0
+            nc.vector.tensor_tensor(
+                out=tt[:, a0:a1, :],
+                in0=pos_f[:, a0:a1].unsqueeze(2).to_broadcast([P, na, PAIRS]),
+                in1=gt[:].unsqueeze(1).to_broadcast([P, na, PAIRS]),
+                op=ALU.mult,
+            )
+            nc.vector.tensor_copy(out=n_s[:, a0:a1, :], in_=tt[:, a0:a1, :])
+            nc.vector.tensor_scalar_add(out=n_c[:, a0:a1, :], in0=tt[:, a0:a1, :], scalar1=0.25)
+            nc.vector.tensor_tensor(out=fr[:, 2, a0:a1, :], in0=tt[:, a0:a1, :], in1=n_s[:, a0:a1, :], op=ALU.subtract)
+            nc.vector.scalar_tensor_tensor(
+                out=fr[:, 1, a0:a1, :], in0=tt[:, a0:a1, :], scalar=0.25, in1=n_c[:, a0:a1, :],
+                op0=ALU.add, op1=ALU.subtract,
+            )
+            nc.vector.tensor_tensor(out=fr[:, 0, a0:a1, :], in0=n_s[:, a0:a1, :], in1=tt[:, a0:a1, :], op=ALU.subtract)
+            for f in range(2):
+                nc.scalar.activation(
+                    out=trig[:, a0:a1, HD * f : HD * f + HD].rearrange("p a (j e) -> p a j e", e=2),
+                    in_=fr[:, 1 - f : 3 - f, a0:a1, :].rearrange("p e a j -> p a j e"),
+                    func=ACT.Sin,
+                    scale=2.0 * math.pi,
+                )
+        lnw4 = const.tile([P, PACK], F32)
+        nc.vector.tensor_copy(out=lnw4[:], in_=lnw_b[:])
+
+        for i in range(0, EARLY, 2):
+            stage_rsqrt(i, 2)
+
+        wg = const.tile([P, F, PACK], BF16, align_bytes=64)
+        wc = const.tile([P, F], U32, align_bytes=64)
+        ws = const.tile([P, F], U8, align_bytes=64)
+        wg_qk = wg[:, 0:QK, :].rearrange("p (h f j) t -> p f h j t", f=2, j=PAIRS)
+        wr_qk = wr[:, :, 0:QK].rearrange("p t (h j f) -> p f h j t", f=2, j=PAIRS)
+        for f in range(2):
+            nc.vector.tensor_copy(out=wg_qk[:, f, :, :, :], in_=wr_qk[:, f, :, :, :])
+        nc.vector.tensor_copy(out=wg[:, QK:F, :], in_=wr[:, :, QK:F].rearrange("p t n -> p n t"))
+
+        wdup = const.tile([P, 2, 2 * HD], F32)
+        for q in range(2):
+            nc.vector.tensor_copy(
+                out=wdup[:, q, :].rearrange("p (f j e) -> p f j e", f=2, e=2),
+                in_=wn[:, q, :].rearrange("p (j f) -> p f j", f=2).unsqueeze(3).to_broadcast([P, 2, PAIRS, 2]),
+            )
+
+        tab = const.tile([P, A, 2, 2 * HD], F32)
+
+        def build_tables(ap):
+            nc.vector.tensor_tensor(
+                out=tab[:, 2 * ap : 2 * ap + 2, :, :],
+                in0=trig[:, 2 * ap : 2 * ap + 2, :].unsqueeze(2).to_broadcast([P, 2, 2, 2 * HD]),
+                in1=wdup[:].unsqueeze(1).to_broadcast([P, 2, 2, 2 * HD]),
+                op=ALU.mult,
+            )
+
+        for c in (1, 0):
+            nc.vector.quantize_mx(
+                out=wc[:, BANK * c : BANK * c + BANK].bitcast(FP8X4),
+                scales=ws[:, BANK * c : BANK * c + BANK],
+                in_=wg[:, BANK * c : BANK * c + BANK, :].rearrange("p n t -> p (n t)"),
+            )
+        build_tables(0)
+
+        def stage_scale(i):
+            xt = xin[i // 2][:, i % 2, :].rearrange("p (c t) -> p t c", t=PACK)
+            xs = xs_pool.tile([P, PACK, P], F32)
+            if i % 2 == 0:
+                nc.gpsimd.tensor_scalar(
+                    out=xs[:], in0=xt, scalar1=rx[:, i : i + 1], scalar2=0.0, op0=ALU.mult, op1=ALU.add
+                )
+            else:
+                nc.scalar.activation(out=xs[:], in_=xt, func=ACT.Copy, scale=rx[:, i : i + 1])
+            st[("xs", i)] = xs
+
+        def stage_transpose(i):
+            xs = st[("xs", i)]
+            xT = ps_t.tile([P, PACK, P], F32)
+            for t in range(PACK):
+                nc.tensor.transpose(out=xT[:, t, :], in_=xs[:, t, :], identity=identf[:])
+            st[("xT", i)] = xT
+
+        def stage_round(i):
+            xT = st[("xT", i)]
+            qb, first, nb = batches[i]
+            if i == first:
+                hg = h_pool.tile([P, nb, P, PACK], BF16, align_bytes=64)
+                st[("hg", qb)] = hg
+            hg = st[("hg", qb)]
+            nc.vector.tensor_tensor(
+                out=hg[:, i - first, :, :],
+                in0=xT[:].rearrange("p t r -> p r t"),
+                in1=lnw4[:].unsqueeze(1).to_broadcast([P, P, PACK]),
+                op=ALU.mult,
+            )
+
+        def stage_quantise(qb, nb):
+            hg = st[("hg", qb)]
+            hc = c_pool.tile([P, nb * P], U32, align_bytes=64)
+            hs = c_pool.tile([P, nb * P], U8, align_bytes=64)
+            nc.vector.quantize_mx(
+                out=hc[:].bitcast(FP8X4), scales=hs[:], in_=hg[:].rearrange("p n r t -> p (n r t)")
+            )
+            st[("hc", qb)] = (hc, hs)
+
+        def stage_matmul(i):
+            qb, first, nb = batches[i]
+            hc, hs = st[("hc", qb)]
+            cols = slice(P * (i - first), P * (i - first) + P)
+            psq = ps_mx.tile([P, BANK], F32)
+            pskv = ps_mx.tile([P, BANK], F32)
+            for c, acc in enumerate((psq, pskv)):
+                nc.tensor.matmul_mx(
+                    out=acc[:],
+                    lhsT=hc[:, cols].bitcast(FP8X4),
+                    lhsT_scale=hs[:, cols],
+                    rhs=wc[:, BANK * c : BANK * c + BANK].bitcast(FP8X4),
+                    rhs_scale=ws[:, BANK * c : BANK * c + BANK],
+                    start=True,
+                    stop=True,
+                )
+            st[("ps", i)] = (psq, pskv)
+
+        def head_cols(i, h):
+            psq, pskv = st[("ps", i)]
+            if h < NQ:
+                return psq[:, HD * h : HD * h + HD]
+            return pskv[:, HD * (h - NQ) : HD * (h - NQ) + HD]
+
+        def stage_headnorm(i):
+            u = i % 2
+            if u == 0:
+                o_t = o_pool.tile([P, 2, F], F32)
+                st[("o", i // 2)] = o_t
+            o_t = st[("o", i // 2)]
+            ssh = small.tile([P, NH], F32)
+            junk_h = j_pool.tile([P, NH, HD], BF16)
+            for h in range(NH):
+                nc.scalar.activation(
+                    out=junk_h[:, h, :], in_=head_cols(i, h), func=ACT.Square, accum_out=ssh[:, h : h + 1]
+                )
+            nc.scalar.copy(out=o_t[:, u, QK:F], in_=st[("ps", i)][1][:, BANK - (F - QK) : BANK])
+            rh = small.tile([P, NH], F32)
+            nc.scalar.activation(
+                out=rh[:], in_=ssh[:], func=ACT.Abs_reciprocal_sqrt, scale=1.0 / HD, bias=eps_t[:]
+            )
+            st[("rh", i)] = rh
+
+        def stage_rotate(i):
+            ap, b, u = tile_coords(i)
+            rh = st[("rh", i)]
+            t_t = t_pool.tile([P, NH, 2 * HD], F32)
+            for h in range(NH):
+                nc.vector.scalar_tensor_tensor(
+                    out=t_t[:, h, :].rearrange("p (d e) -> p d e", e=2),
+                    in0=head_cols(i, h).unsqueeze(2).to_broadcast([P, HD, 2]),
+                    scalar=rh[:, h : h + 1],
+                    in1=tab[:, 2 * ap + u, 0 if h < NQ else 1, :].rearrange("p (d e) -> p d e", e=2),
+                    op0=ALU.mult,
+                    op1=ALU.mult,
+                )
+            st[("t", i)] = t_t
+
+        def stage_sum(i):
+            ap, b, u = tile_coords(i)
+            t_t = st[("t", i)]
+            o_t = st[("o", i // 2)]
+            eng = nc.vector if i == NT - 1 else nc.gpsimd
+            eng.tensor_tensor(
+                out=o_t[:, u, 0:QK].rearrange("p (h d) -> p h d", d=HD),
+                in0=t_t[:, :, 0:HD],
+                in1=t_t[:, :, HD : 2 * HD],
+                op=ALU.add,
+            )
+            if i >= NT - 2:
+                us, sl = slice(u, u + 1), slice(2 * ap + u, 2 * ap + u + 1)
+            elif u == 1:
+                us, sl = slice(0, 2), slice(2 * ap, 2 * ap + 2)
+            else:
+                return
+            nc.sync.dma_start(out=o0v[b, :, sl, :], in_=o_t[:, us, 0 : NQ * HD])
+            nc.sync.dma_start(out=o1v[b, :, sl, :], in_=o_t[:, us, NQ * HD : QK])
+            nc.sync.dma_start(out=o2v[b, :, sl, :], in_=o_t[:, us, QK:F])
+
+        def on(stage, i):
+            if 0 <= i < NT:
+                stage(i)
+
+        slots = NT + LAG_QUANT + 1
+        written = 0
+        for step in range(NT + LAG_SUM + 1):
+            due = range(written, min(slots, slots_by_step(step)))
+            written = max(written, min(slots, slots_by_step(step)))
+            on(stage_matmul, step - LAG_MATMUL)
+            on(stage_sum, step - LAG_SUM)
+            on(stage_headnorm, step - LAG_HEADNORM)
+            for s in due:
+                if s >= EARLY:
+                    on(stage_square, s)
+                if s - LAG_RSQRT >= EARLY:
+                    on(stage_rsqrt, s - LAG_RSQRT)
+                on(stage_scale, s - LAG_SCALE)
+                on(stage_transpose, s - LAG_TRANSPOSE)
+                on(stage_round, s - LAG_ROUND)
+            on(stage_rotate, step - LAG_ROTATE)
+            for s in due:
+                i = s - LAG_QUANT
+                if 0 <= i < NT and i == batches[i][1] + batches[i][2] - 1:
+                    stage_quantise(batches[i][0], batches[i][2])
+            if step + 1 < TABLES_AT_START:
+                build_tables(step + 1)
+            elif step % 4 == 0 and TABLES_AT_START <= step // 4 + 2 < A // 2:
+                build_tables(step // 4 + 2)

@@ -83,8 +83,8 @@ def tile_qwen3block_pa_t_kernel(tc, x, ln_w, qkv_w, q_norm_w, k_norm_w, out_0, o
             g = i // 2
             return g // 2, g % 2, i % 2
 
-        lnw_b = const.tile([P, PACK], BF16)
-        nc.scalar.dma_start(out=lnw_b[:], in_=ln_w.rearrange("(p t) -> p t", t=PACK))
+        lnw_bc = const.tile([P, E], BF16)
+        nc.scalar.dma_start(out=lnw_bc[:], in_=ln_w.partition_broadcast(P))
 
         xin = {}
         wr = const.tile([P, PACK, F], BF16)
@@ -169,8 +169,6 @@ def tile_qwen3block_pa_t_kernel(tc, x, ln_w, qkv_w, q_norm_w, k_norm_w, out_0, o
                     func=ACT.Sin,
                     scale=2.0 * math.pi,
                 )
-        lnw4 = const.tile([P, PACK], F32)
-        nc.vector.tensor_copy(out=lnw4[:], in_=lnw_b[:])
 
         for i in range(0, EARLY, 2):
             stage_rsqrt(i, 2)
@@ -210,21 +208,18 @@ def tile_qwen3block_pa_t_kernel(tc, x, ln_w, qkv_w, q_norm_w, k_norm_w, out_0, o
         build_tables(0)
 
         def stage_scale(i):
-            xt = xin[i // 2][:, i % 2, :].rearrange("p (c t) -> p t c", t=PACK)
-            xs = xs_pool.tile([P, PACK, P], F32)
-            if i % 2 == 0:
-                nc.gpsimd.tensor_scalar(
-                    out=xs[:], in0=xt, scalar1=rx[:, i : i + 1], scalar2=0.0, op0=ALU.mult, op1=ALU.add
-                )
-            else:
-                nc.scalar.activation(out=xs[:], in_=xt, func=ACT.Copy, scale=rx[:, i : i + 1])
+            xt = xin[i // 2][:, i % 2, :]
+            xs = xs_pool.tile([P, E], BF16)
+            nc.vector.scalar_tensor_tensor(
+                out=xs[:], in0=xt, scalar=rx[:, i : i + 1], in1=lnw_bc[:], op0=ALU.mult, op1=ALU.mult
+            )
             st[("xs", i)] = xs
 
         def stage_transpose(i):
-            xs = st[("xs", i)]
+            words = st[("xs", i)][:].bitcast(F32)
             xT = ps_t.tile([P, PACK, P], F32)
-            for t in range(PACK):
-                nc.tensor.transpose(out=xT[:, t, :], in_=xs[:, t, :], identity=identf[:])
+            for u in range(2):
+                nc.tensor.transpose(out=xT[:, u, :], in_=words[:, u : E // 2 : 2], identity=identf[:])
             st[("xT", i)] = xT
 
         def stage_round(i):
@@ -234,12 +229,7 @@ def tile_qwen3block_pa_t_kernel(tc, x, ln_w, qkv_w, q_norm_w, k_norm_w, out_0, o
                 hg = h_pool.tile([P, nb, P, PACK], BF16, align_bytes=64)
                 st[("hg", qb)] = hg
             hg = st[("hg", qb)]
-            nc.vector.tensor_tensor(
-                out=hg[:, i - first, :, :],
-                in0=xT[:].rearrange("p t r -> p r t"),
-                in1=lnw4[:].unsqueeze(1).to_broadcast([P, P, PACK]),
-                op=ALU.mult,
-            )
+            nc.scalar.copy(out=hg[:, i - first, :, :].bitcast(F32), in_=xT[:, 0:2, :].rearrange("p u r -> p r u"))
 
         def stage_quantise(qb, nb):
             hg = st[("hg", qb)]

@@ -143,9 +143,11 @@ def tile_qwen3block_pa_t_kernel(tc, x, ln_w, qkv_w, q_norm_w, k_norm_w, out_0, o
 
         tt = const.tile([P, A, PAIRS], F32)
         n_s = const.tile([P, A, PAIRS], I32)
-        n_c = const.tile([P, A, PAIRS], I32)
-        fr = const.tile([P, 3, A, PAIRS], F32)
-        trig = const.tile([P, A, 2 * HD], F32)
+        fr = const.tile([P, A, PAIRS], F32)
+        af = const.tile([P, A, PAIRS], F32)
+        cs = const.tile([P, A, 2, PAIRS], F32)
+        halfpi = const.tile([P, 1], F32)
+        nc.vector.tensor_scalar_mul(out=halfpi[:], in0=one1[:], scalar1=math.pi / 2.0)
         for a0, a1 in ((0, A // 2), (A // 2, A)):
             na = a1 - a0
             nc.vector.tensor_tensor(
@@ -155,20 +157,12 @@ def tile_qwen3block_pa_t_kernel(tc, x, ln_w, qkv_w, q_norm_w, k_norm_w, out_0, o
                 op=ALU.mult,
             )
             nc.vector.tensor_copy(out=n_s[:, a0:a1, :], in_=tt[:, a0:a1, :])
-            nc.vector.tensor_scalar_add(out=n_c[:, a0:a1, :], in0=tt[:, a0:a1, :], scalar1=0.25)
-            nc.vector.tensor_tensor(out=fr[:, 2, a0:a1, :], in0=tt[:, a0:a1, :], in1=n_s[:, a0:a1, :], op=ALU.subtract)
-            nc.vector.scalar_tensor_tensor(
-                out=fr[:, 1, a0:a1, :], in0=tt[:, a0:a1, :], scalar=0.25, in1=n_c[:, a0:a1, :],
-                op0=ALU.add, op1=ALU.subtract,
+            nc.vector.tensor_tensor(out=fr[:, a0:a1, :], in0=tt[:, a0:a1, :], in1=n_s[:, a0:a1, :], op=ALU.subtract)
+            nc.scalar.activation(out=af[:, a0:a1, :], in_=fr[:, a0:a1, :], func=ACT.Abs)
+            nc.scalar.activation(
+                out=cs[:, a0:a1, 0, :], in_=af[:, a0:a1, :], func=ACT.Sin, scale=-2.0 * math.pi, bias=halfpi[:]
             )
-            nc.vector.tensor_tensor(out=fr[:, 0, a0:a1, :], in0=n_s[:, a0:a1, :], in1=tt[:, a0:a1, :], op=ALU.subtract)
-            for f in range(2):
-                nc.scalar.activation(
-                    out=trig[:, a0:a1, HD * f : HD * f + HD].rearrange("p a (j e) -> p a j e", e=2),
-                    in_=fr[:, 1 - f : 3 - f, a0:a1, :].rearrange("p e a j -> p a j e"),
-                    func=ACT.Sin,
-                    scale=2.0 * math.pi,
-                )
+            nc.scalar.activation(out=cs[:, a0:a1, 1, :], in_=fr[:, a0:a1, :], func=ACT.Sin, scale=2.0 * math.pi)
 
         for i in range(0, EARLY, 2):
             stage_rsqrt(i, 2)
@@ -182,22 +176,31 @@ def tile_qwen3block_pa_t_kernel(tc, x, ln_w, qkv_w, q_norm_w, k_norm_w, out_0, o
             nc.vector.tensor_copy(out=wg_qk[:, f, :, :, :], in_=wr_qk[:, f, :, :, :])
         nc.vector.tensor_copy(out=wg[:, QK:F, :], in_=wr[:, :, QK:F].rearrange("p t n -> p n t"))
 
-        wdup = const.tile([P, 2, 2 * HD], F32)
+        wsg = const.tile([P, 2, 2, 2, PAIRS], F32)
         for q in range(2):
             nc.vector.tensor_copy(
-                out=wdup[:, q, :].rearrange("p (f j e) -> p f j e", f=2, e=2),
-                in_=wn[:, q, :].rearrange("p (j f) -> p f j", f=2).unsqueeze(3).to_broadcast([P, 2, PAIRS, 2]),
+                out=wsg[:, q, :, :, :],
+                in_=wn[:, q, :].rearrange("p (j f) -> p f j", f=2).unsqueeze(1).to_broadcast([P, 2, 2, PAIRS]),
             )
+        nc.vector.tensor_scalar_mul(out=wsg[:, :, 0, 1, :], in0=wsg[:, :, 0, 1, :], scalar1=-1.0)
 
-        tab = const.tile([P, A, 2, 2 * HD], F32)
+        tab = const.tile([P, A, 2, 2, HD], F32)
 
         def build_tables(ap):
+            a = slice(2 * ap, 2 * ap + 2)
             nc.vector.tensor_tensor(
-                out=tab[:, 2 * ap : 2 * ap + 2, :, :],
-                in0=trig[:, 2 * ap : 2 * ap + 2, :].unsqueeze(2).to_broadcast([P, 2, 2, 2 * HD]),
-                in1=wdup[:].unsqueeze(1).to_broadcast([P, 2, 2, 2 * HD]),
+                out=tab[:, a, :, 0, :],
+                in0=cs[:, a, :, :].rearrange("p a c j -> p a (c j)").unsqueeze(2).to_broadcast([P, 2, 2, HD]),
+                in1=wsg[:, :, 0, :, :].rearrange("p q f j -> p q (f j)").unsqueeze(1).to_broadcast([P, 2, 2, HD]),
                 op=ALU.mult,
             )
+            for f in range(2):
+                nc.vector.tensor_tensor(
+                    out=tab[:, a, :, 1, PAIRS * f : PAIRS * f + PAIRS],
+                    in0=cs[:, a, 1 - f, :].unsqueeze(2).to_broadcast([P, 2, 2, PAIRS]),
+                    in1=wsg[:, :, 1, f, :].unsqueeze(1).to_broadcast([P, 2, 2, PAIRS]),
+                    op=ALU.mult,
+                )
 
         for c in (1, 0):
             nc.vector.quantize_mx(
@@ -292,7 +295,7 @@ def tile_qwen3block_pa_t_kernel(tc, x, ln_w, qkv_w, q_norm_w, k_norm_w, out_0, o
                     out=t_t[:, h, :].rearrange("p (d e) -> p d e", e=2),
                     in0=head_cols(i, h).unsqueeze(2).to_broadcast([P, HD, 2]),
                     scalar=rh[:, h : h + 1],
-                    in1=tab[:, 2 * ap + u, 0 if h < NQ else 1, :].rearrange("p (d e) -> p d e", e=2),
+                    in1=tab[:, 2 * ap + u, 0 if h < NQ else 1, :, :].rearrange("p e d -> p d e"),
                     op0=ALU.mult,
                     op1=ALU.mult,
                 )

@@ -42,7 +42,8 @@ LAG_HEADNORM = 2
 LAG_ROTATE = 3
 LAG_SUM = 4
 LEAD = LAG_QUANT + max(QUANT_BATCH)
-TABLES_AT_START = 4
+TABLES_AT_START = 5
+FIRST_ANGLES = 4
 
 
 def quant_batches():
@@ -83,12 +84,17 @@ def tile_qwen3block_pa_t_kernel(tc, x, ln_w, qkv_w, q_norm_w, k_norm_w, out_0, o
             g = i // 2
             return g // 2, g % 2, i % 2
 
-        lnw_bc = const.tile([P, E], BF16)
-        nc.scalar.dma_start(out=lnw_bc[:], in_=ln_w.partition_broadcast(P))
+        st = {}
+        batches = quant_batches()
+
+        rows = const.tile([P, E + 2 * HD], BF16)
+        nc.gpsimd.memset(rows[:], 0.0)
+        nc.sync.dma_start(out=rows[0:1, 0:E], in_=ln_w.rearrange("(o k) -> o k", o=1))
+        nc.sync.dma_start(out=rows[0:1, E : E + HD], in_=q_norm_w.rearrange("(o k) -> o k", o=1))
+        nc.sync.dma_start(out=rows[0:1, E + HD : E + 2 * HD], in_=k_norm_w.rearrange("(o k) -> o k", o=1))
 
         xin = {}
         wr = const.tile([P, PACK, F], BF16)
-        wn = const.tile([P, 2, HD], BF16)
         for g in range(NT // 2):
             ap, b = g // 2, g % 2
             xg = const.tile([P, 2, E], BF16, name="xg%d" % g)
@@ -96,34 +102,22 @@ def tile_qwen3block_pa_t_kernel(tc, x, ln_w, qkv_w, q_norm_w, k_norm_w, out_0, o
             xin[g] = xg
             if g == 1:
                 nc.sync.dma_start(out=wr[:], in_=qkv_w.rearrange("(p t) n -> p t n", t=PACK))
-                nc.sync.dma_start(out=wn[:, 0, :], in_=q_norm_w.partition_broadcast(P))
-                nc.sync.dma_start(out=wn[:, 1, :], in_=k_norm_w.partition_broadcast(P))
 
-        ssx = const.tile([P, NT], F32)
-        rx = const.tile([P, NT], F32)
+        ones_b = const.tile([P, P], BF16)
+        nc.vector.memset(ones_b[:], 1.0)
+        one1 = const.tile([P, 1], F32)
+        nc.vector.memset(one1[:], 1.0)
         eps_t = const.tile([P, 1], F32)
         nc.vector.memset(eps_t[:], EPS)
-        st = {}
-        batches = quant_batches()
-
-        def stage_square(i):
-            xt = xin[i // 2][:, i % 2, :]
-            junk_x = j_pool.tile([P, E], BF16)
-            nc.scalar.activation(out=junk_x[:], in_=xt, func=ACT.Square, accum_out=ssx[:, i : i + 1])
-
-        def stage_rsqrt(i, n=1):
-            nc.scalar.activation(
-                out=rx[:, i : i + n], in_=ssx[:, i : i + n], func=ACT.Abs_reciprocal_sqrt,
-                scale=1.0 / E, bias=eps_t[:],
-            )
-
         pos_i = const.tile([P, A], I32)
         nc.gpsimd.iota(pos_i[:], pattern=[[1, A]], base=0, channel_multiplier=A)
         identf = const.tile([P, P], F32)
         make_identity(nc, identf[:])
+        mhalf = const.tile([P, EARLY], F32)
+        nc.gpsimd.memset(mhalf[:], -0.5)
+        junk1 = const.tile([P, 1], F32)
+        nc.scalar.activation(out=junk1[:], in_=one1[:], func=ACT.Sin)
 
-        one1 = const.tile([P, 1], F32)
-        nc.vector.memset(one1[:], 1.0)
         gt = const.tile([P, PAIRS], F32)
         for j in range(4):
             nc.vector.tensor_scalar_mul(
@@ -137,18 +131,38 @@ def tile_qwen3block_pa_t_kernel(tc, x, ln_w, qkv_w, q_norm_w, k_norm_w, out_0, o
                 )
         pos_f = const.tile([P, A], F32)
         nc.vector.tensor_copy(out=pos_f[:], in_=pos_i[:])
+        halfpi = const.tile([P, 1], F32)
+        nc.vector.tensor_scalar_mul(out=halfpi[:], in0=one1[:], scalar1=math.pi / 2.0)
 
-        for i in range(EARLY):
-            stage_square(i)
+        ssx = const.tile([P, NT], F32)
+        rx = const.tile([P, NT], F32)
+        ms = const.tile([P, EARLY], F32)
+
+        def stage_square(i):
+            xt = xin[i // 2][:, i % 2, :]
+            junk_x = j_pool.tile([P, E], BF16)
+            nc.scalar.activation(out=junk_x[:], in_=xt, func=ACT.Square, accum_out=ssx[:, i : i + 1])
+
+        def stage_rsqrt(i):
+            nc.scalar.activation(
+                out=rx[:, i : i + 1], in_=ssx[:, i : i + 1], func=ACT.Abs_reciprocal_sqrt,
+                scale=1.0 / E, bias=eps_t[:],
+            )
+
+        def early_rsqrt(i, n):
+            cols = slice(i, i + n)
+            nc.gpsimd.tensor_scalar(
+                out=ms[:, cols], in0=ssx[:, cols], scalar1=1.0 / E, scalar2=EPS, op0=ALU.mult, op1=ALU.add
+            )
+            nc.gpsimd.tensor_tensor(out=rx[:, cols], in0=ms[:, cols], in1=mhalf[:, cols], op=ALU.pow)
 
         tt = const.tile([P, A, PAIRS], F32)
         n_s = const.tile([P, A, PAIRS], I32)
         fr = const.tile([P, A, PAIRS], F32)
         af = const.tile([P, A, PAIRS], F32)
         cs = const.tile([P, A, 2, PAIRS], F32)
-        halfpi = const.tile([P, 1], F32)
-        nc.vector.tensor_scalar_mul(out=halfpi[:], in0=one1[:], scalar1=math.pi / 2.0)
-        for a0, a1 in ((0, A // 2), (A // 2, A)):
+
+        def reduce_angles(a0, a1):
             na = a1 - a0
             nc.vector.tensor_tensor(
                 out=tt[:, a0:a1, :],
@@ -158,57 +172,71 @@ def tile_qwen3block_pa_t_kernel(tc, x, ln_w, qkv_w, q_norm_w, k_norm_w, out_0, o
             )
             nc.vector.tensor_copy(out=n_s[:, a0:a1, :], in_=tt[:, a0:a1, :])
             nc.vector.tensor_tensor(out=fr[:, a0:a1, :], in0=tt[:, a0:a1, :], in1=n_s[:, a0:a1, :], op=ALU.subtract)
+
+        def sines(a0, a1):
             nc.scalar.activation(out=af[:, a0:a1, :], in_=fr[:, a0:a1, :], func=ACT.Abs)
             nc.scalar.activation(
                 out=cs[:, a0:a1, 0, :], in_=af[:, a0:a1, :], func=ACT.Sin, scale=-2.0 * math.pi, bias=halfpi[:]
             )
             nc.scalar.activation(out=cs[:, a0:a1, 1, :], in_=fr[:, a0:a1, :], func=ACT.Sin, scale=2.0 * math.pi)
 
-        for i in range(0, EARLY, 2):
-            stage_rsqrt(i, 2)
-
-        wg = const.tile([P, F, PACK], BF16, align_bytes=64)
-        wc = const.tile([P, F], U32, align_bytes=64)
-        ws = const.tile([P, F], U8, align_bytes=64)
-        wg_qk = wg[:, 0:QK, :].rearrange("p (h f j) t -> p f h j t", f=2, j=PAIRS)
-        wr_qk = wr[:, :, 0:QK].rearrange("p t (h j f) -> p f h j t", f=2, j=PAIRS)
-        for f in range(2):
-            nc.vector.tensor_copy(out=wg_qk[:, f, :, :, :], in_=wr_qk[:, f, :, :, :])
-        nc.vector.tensor_copy(out=wg[:, QK:F, :], in_=wr[:, :, QK:F].rearrange("p t n -> p n t"))
-
+        lnw_bc = const.tile([P, E], BF16)
         wsg = const.tile([P, 2, 2, 2, PAIRS], F32)
-        for q in range(2):
-            nc.vector.tensor_copy(
-                out=wsg[:, q, :, :, :],
-                in_=wn[:, q, :].rearrange("p (j f) -> p f j", f=2).unsqueeze(1).to_broadcast([P, 2, 2, PAIRS]),
+
+        def spread_rows():
+            xT = ps_t.tile([P, PACK, P], F32)
+            nc.tensor.matmul(
+                out=xT[:].rearrange("p a b -> p (a b)"), lhsT=ones_b[:], rhs=rows[:, 0:E], start=True, stop=True
             )
-        nc.vector.tensor_scalar_mul(out=wsg[:, :, 0, 1, :], in0=wsg[:, :, 0, 1, :], scalar1=-1.0)
+            nc.vector.tensor_copy(out=lnw_bc[:], in_=xT[:].rearrange("p a b -> p (a b)"))
+            xT = ps_t.tile([P, PACK, P], F32)
+            nc.tensor.matmul(
+                out=xT[:, 0:2, :].rearrange("p a b -> p (a b)"), lhsT=ones_b[:], rhs=rows[:, E : E + 2 * HD],
+                start=True, stop=True,
+            )
+            for q in range(2):
+                nc.vector.tensor_copy(
+                    out=wsg[:, q, :, :, :],
+                    in_=xT[:, q, :].rearrange("p (j f) -> p f j", f=2).unsqueeze(1).to_broadcast([P, 2, 2, PAIRS]),
+                )
+            nc.vector.tensor_scalar_mul(out=wsg[:, :, 0, 1, :], in0=wsg[:, :, 0, 1, :], scalar1=-1.0)
 
         tab = const.tile([P, A, 2, 2, HD], F32)
 
-        def build_tables(ap):
+        def table_piece(ap, piece):
             a = slice(2 * ap, 2 * ap + 2)
-            nc.vector.tensor_tensor(
-                out=tab[:, a, :, 0, :],
-                in0=cs[:, a, :, :].rearrange("p a c j -> p a (c j)").unsqueeze(2).to_broadcast([P, 2, 2, HD]),
-                in1=wsg[:, :, 0, :, :].rearrange("p q f j -> p q (f j)").unsqueeze(1).to_broadcast([P, 2, 2, HD]),
-                op=ALU.mult,
-            )
-            for f in range(2):
-                nc.vector.tensor_tensor(
+            if piece == 0:
+                nc.gpsimd.tensor_tensor(
+                    out=tab[:, a, :, 0, :],
+                    in0=cs[:, a, :, :].rearrange("p a c j -> p a (c j)").unsqueeze(2).to_broadcast([P, 2, 2, HD]),
+                    in1=wsg[:, :, 0, :, :].rearrange("p q f j -> p q (f j)").unsqueeze(1).to_broadcast([P, 2, 2, HD]),
+                    op=ALU.mult,
+                )
+            else:
+                f = piece - 1
+                nc.gpsimd.tensor_tensor(
                     out=tab[:, a, :, 1, PAIRS * f : PAIRS * f + PAIRS],
                     in0=cs[:, a, 1 - f, :].unsqueeze(2).to_broadcast([P, 2, 2, PAIRS]),
                     in1=wsg[:, :, 1, f, :].unsqueeze(1).to_broadcast([P, 2, 2, PAIRS]),
                     op=ALU.mult,
                 )
 
-        for c in (1, 0):
-            nc.vector.quantize_mx(
-                out=wc[:, BANK * c : BANK * c + BANK].bitcast(FP8X4),
-                scales=ws[:, BANK * c : BANK * c + BANK],
-                in_=wg[:, BANK * c : BANK * c + BANK, :].rearrange("p n t -> p (n t)"),
-            )
-        build_tables(0)
+        wg = const.tile([P, F, PACK], BF16, align_bytes=64)
+        wc = const.tile([P, F], U32, align_bytes=64)
+        ws = const.tile([P, F], U8, align_bytes=64)
+
+        def weights():
+            wg_qk = wg[:, 0:QK, :].rearrange("p (h f j) t -> p f h j t", f=2, j=PAIRS)
+            wr_qk = wr[:, :, 0:QK].rearrange("p t (h j f) -> p f h j t", f=2, j=PAIRS)
+            for f in range(2):
+                nc.vector.tensor_copy(out=wg_qk[:, f, :, :, :], in_=wr_qk[:, f, :, :, :])
+            nc.vector.tensor_copy(out=wg[:, QK:F, :], in_=wr[:, :, QK:F].rearrange("p t n -> p n t"))
+            for c in range(2):
+                nc.vector.quantize_mx(
+                    out=wc[:, BANK * c : BANK * c + BANK].bitcast(FP8X4),
+                    scales=ws[:, BANK * c : BANK * c + BANK],
+                    in_=wg[:, BANK * c : BANK * c + BANK, :].rearrange("p n t -> p (n t)"),
+                )
 
         def stage_scale(i):
             xt = xin[i // 2][:, i % 2, :]
@@ -326,6 +354,20 @@ def tile_qwen3block_pa_t_kernel(tc, x, ln_w, qkv_w, q_norm_w, k_norm_w, out_0, o
             if 0 <= i < NT:
                 stage(i)
 
+        reduce_angles(0, FIRST_ANGLES)
+        sines(0, FIRST_ANGLES)
+        for i in range(EARLY):
+            stage_square(i)
+        reduce_angles(FIRST_ANGLES, A)
+        sines(FIRST_ANGLES, A)
+        spread_rows()
+        for i in range(0, EARLY, 2):
+            early_rsqrt(i, 2)
+        pieces = [(ap, piece) for ap in range(A // 2) for piece in range(3)]
+        for ap, piece in pieces[: 3 * TABLES_AT_START]:
+            table_piece(ap, piece)
+        later_pieces = pieces[3 * TABLES_AT_START :]
+
         slots = NT + LAG_QUANT + 1
         written = 0
         for step in range(NT + LAG_SUM + 1):
@@ -333,7 +375,10 @@ def tile_qwen3block_pa_t_kernel(tc, x, ln_w, qkv_w, q_norm_w, k_norm_w, out_0, o
             written = max(written, min(slots, slots_by_step(step)))
             on(stage_matmul, step - LAG_MATMUL)
             on(stage_sum, step - LAG_SUM)
+            if step > LAG_SUM and later_pieces:
+                table_piece(*later_pieces.pop(0))
             on(stage_headnorm, step - LAG_HEADNORM)
+            on(stage_rotate, step - LAG_ROTATE)
             for s in due:
                 if s >= EARLY:
                     on(stage_square, s)
@@ -342,12 +387,9 @@ def tile_qwen3block_pa_t_kernel(tc, x, ln_w, qkv_w, q_norm_w, k_norm_w, out_0, o
                 on(stage_scale, s - LAG_SCALE)
                 on(stage_transpose, s - LAG_TRANSPOSE)
                 on(stage_round, s - LAG_ROUND)
-            on(stage_rotate, step - LAG_ROTATE)
+                if s - LAG_SCALE == EARLY - 1:
+                    weights()
             for s in due:
                 i = s - LAG_QUANT
                 if 0 <= i < NT and i == batches[i][1] + batches[i][2] - 1:
                     stage_quantise(batches[i][0], batches[i][2])
-            if step + 1 < TABLES_AT_START:
-                build_tables(step + 1)
-            elif step % 4 == 0 and TABLES_AT_START <= step // 4 + 2 < A // 2:
-                build_tables(step // 4 + 2)

@@ -71,7 +71,8 @@ def tile_qwen3block_pa_t_kernel(tc, x, ln_w, qkv_w, q_norm_w, k_norm_w, out_0, o
         j_pool = ctx.enter_context(tc.tile_pool(name="j_pool", bufs=3))
         t_pool = ctx.enter_context(tc.tile_pool(name="t_pool", bufs=3))
         o_pool = ctx.enter_context(tc.tile_pool(name="o_pool", bufs=4))
-        ps_t = ctx.enter_context(tc.psum_pool(name="ps_t", bufs=2))
+        ps_t = ctx.enter_context(tc.psum_pool(name="ps_t", bufs=1))
+        ps_c = ctx.enter_context(tc.psum_pool(name="ps_c", bufs=1))
         ps_mx = ctx.enter_context(tc.psum_pool(name="ps_mx", bufs=3))
         ctx.enter_context(tc.manual_schedule())
 
@@ -180,15 +181,11 @@ def tile_qwen3block_pa_t_kernel(tc, x, ln_w, qkv_w, q_norm_w, k_norm_w, out_0, o
             )
             nc.scalar.activation(out=cs[:, a0:a1, 1, :], in_=fr[:, a0:a1, :], func=ACT.Sin, scale=2.0 * math.pi)
 
-        lnw_bc = const.tile([P, E], BF16)
+        lnw_bc = ps_c.tile([P, E], F32)
         wsg = const.tile([P, 2, 2, 2, PAIRS], F32)
 
         def spread_rows():
-            xT = ps_t.tile([P, PACK, P], F32)
-            nc.tensor.matmul(
-                out=xT[:].rearrange("p a b -> p (a b)"), lhsT=ones_b[:], rhs=rows[:, 0:E], start=True, stop=True
-            )
-            nc.vector.tensor_copy(out=lnw_bc[:], in_=xT[:].rearrange("p a b -> p (a b)"))
+            nc.tensor.matmul(out=lnw_bc[:], lhsT=ones_b[:], rhs=rows[:, 0:E], start=True, stop=True)
             xT = ps_t.tile([P, PACK, P], F32)
             nc.tensor.matmul(
                 out=xT[:, 0:2, :].rearrange("p a b -> p (a b)"), lhsT=ones_b[:], rhs=rows[:, E : E + 2 * HD],

@@ -41,9 +41,12 @@ LAG_MATMUL = 1
 LAG_HEADNORM = 2
 LAG_ROTATE = 3
 LAG_SUM = 4
-LEAD = LAG_QUANT + max(QUANT_BATCH)
+LEAD = LAG_QUANT + max(QUANT_BATCH) + 1
 TABLES_AT_START = 5
 FIRST_ANGLES = 4
+SUM_HEADS = 6
+QUANT_AFTER = 5
+VECTOR_TABLES = 0
 
 
 def quant_batches():
@@ -57,7 +60,7 @@ def quant_batches():
 
 
 def slots_by_step(step):
-    return min(LAG_QUANT + 1 + 2 * step, step + LEAD)
+    return min(LAG_QUANT + 2 + 2 * step, step + LEAD)
 
 
 def tile_qwen3block_pa_t_kernel(tc, x, ln_w, qkv_w, q_norm_w, k_norm_w, out_0, out_1, out_2):
@@ -114,8 +117,6 @@ def tile_qwen3block_pa_t_kernel(tc, x, ln_w, qkv_w, q_norm_w, k_norm_w, out_0, o
         nc.gpsimd.iota(pos_i[:], pattern=[[1, A]], base=0, channel_multiplier=A)
         identf = const.tile([P, P], F32)
         make_identity(nc, identf[:])
-        mhalf = const.tile([P, EARLY], F32)
-        nc.gpsimd.memset(mhalf[:], -0.5)
         junk1 = const.tile([P, 1], F32)
         nc.scalar.activation(out=junk1[:], in_=one1[:], func=ACT.Sin)
 
@@ -137,7 +138,6 @@ def tile_qwen3block_pa_t_kernel(tc, x, ln_w, qkv_w, q_norm_w, k_norm_w, out_0, o
 
         ssx = const.tile([P, NT], F32)
         rx = const.tile([P, NT], F32)
-        ms = const.tile([P, EARLY], F32)
 
         def stage_square(i):
             xt = xin[i // 2][:, i % 2, :]
@@ -152,10 +152,9 @@ def tile_qwen3block_pa_t_kernel(tc, x, ln_w, qkv_w, q_norm_w, k_norm_w, out_0, o
 
         def early_rsqrt(i, n):
             cols = slice(i, i + n)
-            nc.gpsimd.tensor_scalar(
-                out=ms[:, cols], in0=ssx[:, cols], scalar1=1.0 / E, scalar2=EPS, op0=ALU.mult, op1=ALU.add
+            nc.scalar.activation(
+                out=rx[:, cols], in_=ssx[:, cols], func=ACT.Abs_reciprocal_sqrt, scale=1.0 / E, bias=eps_t[:]
             )
-            nc.gpsimd.tensor_tensor(out=rx[:, cols], in0=ms[:, cols], in1=mhalf[:, cols], op=ALU.pow)
 
         tt = const.tile([P, A, PAIRS], F32)
         n_s = const.tile([P, A, PAIRS], I32)
@@ -200,10 +199,10 @@ def tile_qwen3block_pa_t_kernel(tc, x, ln_w, qkv_w, q_norm_w, k_norm_w, out_0, o
 
         tab = const.tile([P, A, 2, 2, HD], F32)
 
-        def table_piece(ap, piece):
+        def table_piece(ap, piece, eng):
             a = slice(2 * ap, 2 * ap + 2)
             if piece == 0:
-                nc.gpsimd.tensor_tensor(
+                eng.tensor_tensor(
                     out=tab[:, a, :, 0, :],
                     in0=cs[:, a, :, :].rearrange("p a c j -> p a (c j)").unsqueeze(2).to_broadcast([P, 2, 2, HD]),
                     in1=wsg[:, :, 0, :, :].rearrange("p q f j -> p q (f j)").unsqueeze(1).to_broadcast([P, 2, 2, HD]),
@@ -211,7 +210,7 @@ def tile_qwen3block_pa_t_kernel(tc, x, ln_w, qkv_w, q_norm_w, k_norm_w, out_0, o
                 )
             else:
                 f = piece - 1
-                nc.gpsimd.tensor_tensor(
+                eng.tensor_tensor(
                     out=tab[:, a, :, 1, PAIRS * f : PAIRS * f + PAIRS],
                     in0=cs[:, a, 1 - f, :].unsqueeze(2).to_broadcast([P, 2, 2, PAIRS]),
                     in1=wsg[:, :, 1, f, :].unsqueeze(1).to_broadcast([P, 2, 2, PAIRS]),
@@ -311,11 +310,14 @@ def tile_qwen3block_pa_t_kernel(tc, x, ln_w, qkv_w, q_norm_w, k_norm_w, out_0, o
             )
             st[("rh", i)] = rh
 
-        def stage_rotate(i):
+        def stage_rotate(i, h0, h1):
             ap, b, u = tile_coords(i)
             rh = st[("rh", i)]
-            t_t = t_pool.tile([P, NH, 2 * HD], F32)
-            for h in range(NH):
+            if h0 == 0:
+                t_t = t_pool.tile([P, NH, 2 * HD], F32)
+                st[("t", i)] = t_t
+            t_t = st[("t", i)]
+            for h in range(h0, h1):
                 nc.vector.scalar_tensor_tensor(
                     out=t_t[:, h, :].rearrange("p (d e) -> p d e", e=2),
                     in0=head_cols(i, h).unsqueeze(2).to_broadcast([P, HD, 2]),
@@ -324,19 +326,19 @@ def tile_qwen3block_pa_t_kernel(tc, x, ln_w, qkv_w, q_norm_w, k_norm_w, out_0, o
                     op0=ALU.mult,
                     op1=ALU.mult,
                 )
-            st[("t", i)] = t_t
 
         def stage_sum(i):
             ap, b, u = tile_coords(i)
             t_t = st[("t", i)]
             o_t = st[("o", i // 2)]
             eng = nc.vector if i == NT - 1 else nc.gpsimd
-            eng.tensor_tensor(
-                out=o_t[:, u, 0:QK].rearrange("p (h d) -> p h d", d=HD),
-                in0=t_t[:, :, 0:HD],
-                in1=t_t[:, :, HD : 2 * HD],
-                op=ALU.add,
-            )
+            for h0 in range(0, NH, SUM_HEADS):
+                eng.tensor_tensor(
+                    out=o_t[:, u, HD * h0 : HD * (h0 + SUM_HEADS)].rearrange("p (h d) -> p h d", d=HD),
+                    in0=t_t[:, h0 : h0 + SUM_HEADS, 0:HD],
+                    in1=t_t[:, h0 : h0 + SUM_HEADS, HD : 2 * HD],
+                    op=ALU.add,
+                )
             if i >= NT - 2:
                 us, sl = slice(u, u + 1), slice(2 * ap + u, 2 * ap + u + 1)
             elif u == 1:
@@ -361,21 +363,30 @@ def tile_qwen3block_pa_t_kernel(tc, x, ln_w, qkv_w, q_norm_w, k_norm_w, out_0, o
         for i in range(0, EARLY, 2):
             early_rsqrt(i, 2)
         pieces = [(ap, piece) for ap in range(A // 2) for piece in range(3)]
-        for ap, piece in pieces[: 3 * TABLES_AT_START]:
-            table_piece(ap, piece)
+        vector_pieces = pieces[: 3 * VECTOR_TABLES]
+        for ap, piece in pieces[3 * VECTOR_TABLES : 3 * TABLES_AT_START]:
+            table_piece(ap, piece, nc.gpsimd)
         later_pieces = pieces[3 * TABLES_AT_START :]
 
+        weights()
         slots = NT + LAG_QUANT + 1
         written = 0
+        pending = []
         for step in range(NT + LAG_SUM + 1):
             due = range(written, min(slots, slots_by_step(step)))
             written = max(written, min(slots, slots_by_step(step)))
             on(stage_matmul, step - LAG_MATMUL)
             on(stage_sum, step - LAG_SUM)
             if step > LAG_SUM and later_pieces:
-                table_piece(*later_pieces.pop(0))
+                table_piece(*later_pieces.pop(0), nc.gpsimd)
             on(stage_headnorm, step - LAG_HEADNORM)
-            on(stage_rotate, step - LAG_ROTATE)
+            if 0 <= step - LAG_ROTATE < NT:
+                stage_rotate(step - LAG_ROTATE, 0, QUANT_AFTER)
+            for qb, nb in pending:
+                stage_quantise(qb, nb)
+            pending = []
+            if 0 <= step - LAG_ROTATE < NT:
+                stage_rotate(step - LAG_ROTATE, QUANT_AFTER, NH)
             for s in due:
                 if s >= EARLY:
                     on(stage_square, s)
@@ -384,9 +395,12 @@ def tile_qwen3block_pa_t_kernel(tc, x, ln_w, qkv_w, q_norm_w, k_norm_w, out_0, o
                 on(stage_scale, s - LAG_SCALE)
                 on(stage_transpose, s - LAG_TRANSPOSE)
                 on(stage_round, s - LAG_ROUND)
-                if s - LAG_SCALE == EARLY - 1:
-                    weights()
             for s in due:
                 i = s - LAG_QUANT
                 if 0 <= i < NT and i == batches[i][1] + batches[i][2] - 1:
-                    stage_quantise(batches[i][0], batches[i][2])
+                    if step < LAG_ROTATE:
+                        stage_quantise(batches[i][0], batches[i][2])
+                    else:
+                        pending.append((batches[i][0], batches[i][2]))
+            for ap, piece in vector_pieces[3 * step : 3 * step + 3]:
+                table_piece(ap, piece, nc.vector)

@@ -31,7 +31,7 @@ EPS = 1e-6
 ROPE_BASE = 1000000.0
 
 QUANT_BATCH = (1, 1, 2, 4, 4, 4, 4, 4, 4, 4)
-EARLY = 4
+EARLY = 2
 LAG_RSQRT = 1
 LAG_SCALE = 2
 LAG_TRANSPOSE = 4
@@ -44,7 +44,7 @@ LAG_SUM = 4
 LEAD = LAG_QUANT + max(QUANT_BATCH) + 1
 TABLES_AT_START = 5
 FIRST_ANGLES = 4
-SUM_HEADS = 6
+HEAD_ORDER = (4, 5, 0, 1, 2, 3)
 QUANT_AFTER = 5
 VECTOR_TABLES = 0
 
@@ -74,9 +74,10 @@ def tile_qwen3block_pa_t_kernel(tc, x, ln_w, qkv_w, q_norm_w, k_norm_w, out_0, o
         j_pool = ctx.enter_context(tc.tile_pool(name="j_pool", bufs=3))
         t_pool = ctx.enter_context(tc.tile_pool(name="t_pool", bufs=3))
         o_pool = ctx.enter_context(tc.tile_pool(name="o_pool", bufs=4))
-        ps_t = ctx.enter_context(tc.psum_pool(name="ps_t", bufs=1))
+        ps_t = ctx.enter_context(tc.psum_pool(name="ps_t", bufs=2))
         ps_c = ctx.enter_context(tc.psum_pool(name="ps_c", bufs=1))
         ps_mx = ctx.enter_context(tc.psum_pool(name="ps_mx", bufs=3))
+        ps_kv = ctx.enter_context(tc.psum_pool(name="ps_kv", bufs=2))
         ctx.enter_context(tc.manual_schedule())
 
         xv = x.rearrange("b (p a) e -> b p a e", a=A)
@@ -93,9 +94,6 @@ def tile_qwen3block_pa_t_kernel(tc, x, ln_w, qkv_w, q_norm_w, k_norm_w, out_0, o
 
         rows = const.tile([P, E + 2 * HD], BF16)
         nc.gpsimd.memset(rows[:], 0.0)
-        nc.sync.dma_start(out=rows[0:1, 0:E], in_=ln_w.rearrange("(o k) -> o k", o=1))
-        nc.sync.dma_start(out=rows[0:1, E : E + HD], in_=q_norm_w.rearrange("(o k) -> o k", o=1))
-        nc.sync.dma_start(out=rows[0:1, E + HD : E + 2 * HD], in_=k_norm_w.rearrange("(o k) -> o k", o=1))
 
         xin = {}
         wr = const.tile([P, PACK, F], BF16)
@@ -104,6 +102,10 @@ def tile_qwen3block_pa_t_kernel(tc, x, ln_w, qkv_w, q_norm_w, k_norm_w, out_0, o
             xg = const.tile([P, 2, E], BF16, name="xg%d" % g)
             nc.sync.dma_start(out=xg[:], in_=xv[b, :, 2 * ap : 2 * ap + 2, :])
             xin[g] = xg
+            if g == 0:
+                nc.sync.dma_start(out=rows[0:1, 0:E], in_=ln_w.rearrange("(o k) -> o k", o=1))
+                nc.sync.dma_start(out=rows[0:1, E : E + HD], in_=q_norm_w.rearrange("(o k) -> o k", o=1))
+                nc.sync.dma_start(out=rows[0:1, E + HD : E + 2 * HD], in_=k_norm_w.rearrange("(o k) -> o k", o=1))
             if g == 1:
                 nc.sync.dma_start(out=wr[:], in_=qkv_w.rearrange("(p t) n -> p t n", t=PACK))
 
@@ -272,7 +274,7 @@ def tile_qwen3block_pa_t_kernel(tc, x, ln_w, qkv_w, q_norm_w, k_norm_w, out_0, o
             hc, hs = st[("hc", qb)]
             cols = slice(P * (i - first), P * (i - first) + P)
             psq = ps_mx.tile([P, BANK], F32)
-            pskv = ps_mx.tile([P, BANK], F32)
+            pskv = ps_kv.tile([P, BANK], F32)
             for c, acc in enumerate((psq, pskv)):
                 nc.tensor.matmul_mx(
                     out=acc[:],
@@ -304,6 +306,9 @@ def tile_qwen3block_pa_t_kernel(tc, x, ln_w, qkv_w, q_norm_w, k_norm_w, out_0, o
                     out=junk_h[:, h, :], in_=head_cols(i, h), func=ACT.Square, accum_out=ssh[:, h : h + 1]
                 )
             nc.scalar.copy(out=o_t[:, u, QK:F], in_=st[("ps", i)][1][:, BANK - (F - QK) : BANK])
+            if i >= NT - 2:
+                ap, b, u = tile_coords(i)
+                nc.sync.dma_start(out=o2v[b, :, 2 * ap + u : 2 * ap + u + 1, :], in_=o_t[:, u : u + 1, QK:F])
             rh = small.tile([P, NH], F32)
             nc.scalar.activation(
                 out=rh[:], in_=ssh[:], func=ACT.Abs_reciprocal_sqrt, scale=1.0 / HD, bias=eps_t[:]
@@ -317,7 +322,7 @@ def tile_qwen3block_pa_t_kernel(tc, x, ln_w, qkv_w, q_norm_w, k_norm_w, out_0, o
                 t_t = t_pool.tile([P, NH, 2 * HD], F32)
                 st[("t", i)] = t_t
             t_t = st[("t", i)]
-            for h in range(h0, h1):
+            for h in HEAD_ORDER[h0:h1]:
                 nc.vector.scalar_tensor_tensor(
                     out=t_t[:, h, :].rearrange("p (d e) -> p d e", e=2),
                     in0=head_cols(i, h).unsqueeze(2).to_broadcast([P, HD, 2]),
@@ -327,18 +332,21 @@ def tile_qwen3block_pa_t_kernel(tc, x, ln_w, qkv_w, q_norm_w, k_norm_w, out_0, o
                     op1=ALU.mult,
                 )
 
-        def stage_sum(i):
-            ap, b, u = tile_coords(i)
+        def sum_heads(i, h0, h1, eng):
+            u = i % 2
             t_t = st[("t", i)]
             o_t = st[("o", i // 2)]
-            eng = nc.vector if i == NT - 1 else nc.gpsimd
-            for h0 in range(0, NH, SUM_HEADS):
-                eng.tensor_tensor(
-                    out=o_t[:, u, HD * h0 : HD * (h0 + SUM_HEADS)].rearrange("p (h d) -> p h d", d=HD),
-                    in0=t_t[:, h0 : h0 + SUM_HEADS, 0:HD],
-                    in1=t_t[:, h0 : h0 + SUM_HEADS, HD : 2 * HD],
-                    op=ALU.add,
-                )
+            eng.tensor_tensor(
+                out=o_t[:, u, HD * h0 : HD * h1].rearrange("p (h d) -> p h d", d=HD),
+                in0=t_t[:, h0:h1, 0:HD],
+                in1=t_t[:, h0:h1, HD : 2 * HD],
+                op=ALU.add,
+            )
+
+        def stage_sum(i):
+            ap, b, u = tile_coords(i)
+            o_t = st[("o", i // 2)]
+            sum_heads(i, 0, NH, nc.gpsimd)
             if i >= NT - 2:
                 us, sl = slice(u, u + 1), slice(2 * ap + u, 2 * ap + u + 1)
             elif u == 1:
@@ -347,7 +355,28 @@ def tile_qwen3block_pa_t_kernel(tc, x, ln_w, qkv_w, q_norm_w, k_norm_w, out_0, o
                 return
             nc.sync.dma_start(out=o0v[b, :, sl, :], in_=o_t[:, us, 0 : NQ * HD])
             nc.sync.dma_start(out=o1v[b, :, sl, :], in_=o_t[:, us, NQ * HD : QK])
-            nc.sync.dma_start(out=o2v[b, :, sl, :], in_=o_t[:, us, QK:F])
+            if i < NT - 2:
+                nc.sync.dma_start(out=o2v[b, :, sl, :], in_=o_t[:, us, QK:F])
+
+        def last_tile():
+            i = NT - 1
+            ap, b, u = tile_coords(i)
+            o_t = st[("o", i // 2)]
+            sl = slice(2 * ap + u, 2 * ap + u + 1)
+
+            def add_and_store(h0):
+                sum_heads(i, h0, h0 + 2, nc.vector)
+                if h0 < NQ:
+                    nc.sync.dma_start(out=o0v[b, :, sl, HD * h0 : HD * (h0 + 2)], in_=o_t[:, u : u + 1, HD * h0 : HD * (h0 + 2)])
+                else:
+                    nc.sync.dma_start(out=o1v[b, :, sl, :], in_=o_t[:, u : u + 1, NQ * HD : QK])
+
+            stage_rotate(i, 0, 2)
+            stage_rotate(i, 2, 4)
+            add_and_store(HEAD_ORDER[0])
+            stage_rotate(i, 4, 6)
+            add_and_store(HEAD_ORDER[2])
+            add_and_store(HEAD_ORDER[4])
 
         def on(stage, i):
             if 0 <= i < NT:
@@ -376,16 +405,19 @@ def tile_qwen3block_pa_t_kernel(tc, x, ln_w, qkv_w, q_norm_w, k_norm_w, out_0, o
             due = range(written, min(slots, slots_by_step(step)))
             written = max(written, min(slots, slots_by_step(step)))
             on(stage_matmul, step - LAG_MATMUL)
-            on(stage_sum, step - LAG_SUM)
+            if step - LAG_SUM < NT - 1:
+                on(stage_sum, step - LAG_SUM)
             if step > LAG_SUM and later_pieces:
                 table_piece(*later_pieces.pop(0), nc.gpsimd)
             on(stage_headnorm, step - LAG_HEADNORM)
-            if 0 <= step - LAG_ROTATE < NT:
+            if step - LAG_ROTATE == NT - 1:
+                last_tile()
+            if 0 <= step - LAG_ROTATE < NT - 1:
                 stage_rotate(step - LAG_ROTATE, 0, QUANT_AFTER)
             for qb, nb in pending:
                 stage_quantise(qb, nb)
             pending = []
-            if 0 <= step - LAG_ROTATE < NT:
+            if 0 <= step - LAG_ROTATE < NT - 1:
                 stage_rotate(step - LAG_ROTATE, QUANT_AFTER, NH)
             for s in due:
                 if s >= EARLY:

@@ -30,19 +30,20 @@ BANK = 512
 EPS = 1e-6
 ROPE_BASE = 1000000.0
 
-QUANT_BATCH = (1, 1, 2, 4, 4, 4, 4, 4, 4, 4)
+QUANT_BATCH = (2, 2, 4, 4, 4, 4, 4, 4, 4)
 EARLY = 2
-LAG_RSQRT = 1
-LAG_SCALE = 2
-LAG_TRANSPOSE = 4
-LAG_ROUND = 5
+LAG_RSQRT = 2
+LAG_SCALE = 3
+LAG_TRANSPOSE = 5
+LAG_ROUND = 6
 LAG_QUANT = 6
 LAG_MATMUL = 1
 LAG_HEADNORM = 2
 LAG_ROTATE = 3
 LAG_SUM = 4
 LEAD = LAG_QUANT + max(QUANT_BATCH) + 1
-TABLES_AT_START = 5
+TABLES_AT_START = 3
+TABLE_BLOCK = 4
 FIRST_ANGLES = 4
 HEAD_ORDER = (4, 5, 0, 1, 2, 3)
 QUANT_AFTER = 5
@@ -148,7 +149,7 @@ def tile_qwen3block_pa_t_kernel(tc, x, ln_w, qkv_w, q_norm_w, k_norm_w, out_0, o
 
         def stage_rsqrt(i):
             nc.scalar.activation(
-                out=rx[:, i : i + 1], in_=ssx[:, i : i + 1], func=ACT.Abs_reciprocal_sqrt,
+                out=rx[:, i : i + 2], in_=ssx[:, i : i + 2], func=ACT.Abs_reciprocal_sqrt,
                 scale=1.0 / E, bias=eps_t[:],
             )
 
@@ -201,21 +202,21 @@ def tile_qwen3block_pa_t_kernel(tc, x, ln_w, qkv_w, q_norm_w, k_norm_w, out_0, o
 
         tab = const.tile([P, A, 2, 2, HD], F32)
 
-        def table_piece(ap, piece, eng):
-            a = slice(2 * ap, 2 * ap + 2)
+        def table_piece(blk, piece, eng):
+            a = slice(TABLE_BLOCK * blk, TABLE_BLOCK * (blk + 1))
             if piece == 0:
                 eng.tensor_tensor(
                     out=tab[:, a, :, 0, :],
-                    in0=cs[:, a, :, :].rearrange("p a c j -> p a (c j)").unsqueeze(2).to_broadcast([P, 2, 2, HD]),
-                    in1=wsg[:, :, 0, :, :].rearrange("p q f j -> p q (f j)").unsqueeze(1).to_broadcast([P, 2, 2, HD]),
+                    in0=cs[:, a, :, :].rearrange("p a c j -> p a (c j)").unsqueeze(2).to_broadcast([P, TABLE_BLOCK, 2, HD]),
+                    in1=wsg[:, :, 0, :, :].rearrange("p q f j -> p q (f j)").unsqueeze(1).to_broadcast([P, TABLE_BLOCK, 2, HD]),
                     op=ALU.mult,
                 )
             else:
                 f = piece - 1
                 eng.tensor_tensor(
                     out=tab[:, a, :, 1, PAIRS * f : PAIRS * f + PAIRS],
-                    in0=cs[:, a, 1 - f, :].unsqueeze(2).to_broadcast([P, 2, 2, PAIRS]),
-                    in1=wsg[:, :, 1, f, :].unsqueeze(1).to_broadcast([P, 2, 2, PAIRS]),
+                    in0=cs[:, a, 1 - f, :].unsqueeze(2).to_broadcast([P, TABLE_BLOCK, 2, PAIRS]),
+                    in1=wsg[:, :, 1, f, :].unsqueeze(1).to_broadcast([P, TABLE_BLOCK, 2, PAIRS]),
                     op=ALU.mult,
                 )
 
@@ -245,10 +246,11 @@ def tile_qwen3block_pa_t_kernel(tc, x, ln_w, qkv_w, q_norm_w, k_norm_w, out_0, o
             st[("xs", i)] = xs
 
         def stage_transpose(i):
-            words = st[("xs", i)][:].bitcast(F32)
-            xT = ps_t.tile([P, PACK, P], F32)
-            for u in range(2):
-                nc.tensor.transpose(out=xT[:, u, :], in_=words[:, u : E // 2 : 2], identity=identf[:])
+            xT = ps_t.tile([P, 2, 2, P], F32)
+            for n in range(2):
+                words = st[("xs", i + n)][:].bitcast(F32)
+                for u in range(2):
+                    nc.tensor.transpose(out=xT[:, n, u, :], in_=words[:, u : E // 2 : 2], identity=identf[:])
             st[("xT", i)] = xT
 
         def stage_round(i):
@@ -258,7 +260,9 @@ def tile_qwen3block_pa_t_kernel(tc, x, ln_w, qkv_w, q_norm_w, k_norm_w, out_0, o
                 hg = h_pool.tile([P, nb, P, PACK], BF16, align_bytes=64)
                 st[("hg", qb)] = hg
             hg = st[("hg", qb)]
-            nc.scalar.copy(out=hg[:, i - first, :, :].bitcast(F32), in_=xT[:, 0:2, :].rearrange("p u r -> p r u"))
+            nc.scalar.copy(
+                out=hg[:, i - first : i - first + 2, :, :].bitcast(F32), in_=xT[:].rearrange("p n u r -> p n r u")
+            )
 
         def stage_quantise(qb, nb):
             hg = st[("hg", qb)]
@@ -391,7 +395,7 @@ def tile_qwen3block_pa_t_kernel(tc, x, ln_w, qkv_w, q_norm_w, k_norm_w, out_0, o
         spread_rows()
         for i in range(0, EARLY, 2):
             early_rsqrt(i, 2)
-        pieces = [(ap, piece) for ap in range(A // 2) for piece in range(3)]
+        pieces = [(blk, piece) for blk in range(A // TABLE_BLOCK) for piece in range(3)]
         vector_pieces = pieces[: 3 * VECTOR_TABLES]
         for ap, piece in pieces[3 * VECTOR_TABLES : 3 * TABLES_AT_START]:
             table_piece(ap, piece, nc.gpsimd)
@@ -422,11 +426,13 @@ def tile_qwen3block_pa_t_kernel(tc, x, ln_w, qkv_w, q_norm_w, k_norm_w, out_0, o
             for s in due:
                 if s >= EARLY:
                     on(stage_square, s)
-                if s - LAG_RSQRT >= EARLY:
+                if s - LAG_RSQRT >= EARLY and s % 2 == 0:
                     on(stage_rsqrt, s - LAG_RSQRT)
                 on(stage_scale, s - LAG_SCALE)
-                on(stage_transpose, s - LAG_TRANSPOSE)
-                on(stage_round, s - LAG_ROUND)
+                if s % 2 == 1:
+                    on(stage_transpose, s - LAG_TRANSPOSE)
+                else:
+                    on(stage_round, s - LAG_ROUND)
             for s in due:
                 i = s - LAG_QUANT
                 if 0 <= i < NT and i == batches[i][1] + batches[i][2] - 1:

@@ -47,7 +47,7 @@ TABLE_BLOCK = 4
 FIRST_ANGLES = 4
 HEAD_ORDER = (4, 5, 0, 1, 2, 3)
 QUANT_AFTER = 5
-VECTOR_TABLES = 0
+VECTOR_TABLES = 1
 
 
 def quant_batches():
@@ -73,7 +73,7 @@ def tile_qwen3block_pa_t_kernel(tc, x, ln_w, qkv_w, q_norm_w, k_norm_w, out_0, o
         h_pool = ctx.enter_context(tc.tile_pool(name="h_pool", bufs=3))
         c_pool = ctx.enter_context(tc.tile_pool(name="c_pool", bufs=3))
         j_pool = ctx.enter_context(tc.tile_pool(name="j_pool", bufs=3))
-        t_pool = ctx.enter_context(tc.tile_pool(name="t_pool", bufs=3))
+        t_pool = ctx.enter_context(tc.tile_pool(name="t_pool", bufs=5))
         o_pool = ctx.enter_context(tc.tile_pool(name="o_pool", bufs=4))
         ps_t = ctx.enter_context(tc.psum_pool(name="ps_t", bufs=2))
         ps_c = ctx.enter_context(tc.psum_pool(name="ps_c", bufs=1))

@@ -193,12 +193,10 @@ def tile_qwen3block_pa_t_kernel(tc, x, ln_w, qkv_w, q_norm_w, k_norm_w, out_0, o
                 out=xT[:, 0:2, :].rearrange("p a b -> p (a b)"), lhsT=ones_b[:], rhs=rows[:, E : E + 2 * HD],
                 start=True, stop=True,
             )
-            for q in range(2):
-                nc.vector.tensor_copy(
-                    out=wsg[:, q, :, :, :],
-                    in_=xT[:, q, :].rearrange("p (j f) -> p f j", f=2).unsqueeze(1).to_broadcast([P, 2, 2, PAIRS]),
-                )
-            nc.vector.tensor_scalar_mul(out=wsg[:, :, 0, 1, :], in0=wsg[:, :, 0, 1, :], scalar1=-1.0)
+            gains = xT[:, 0:2, :].rearrange("p q (j f) -> p q f j", f=2)
+            nc.scalar.copy(out=wsg[:, :, 1, :, :], in_=gains)
+            nc.scalar.copy(out=wsg[:, :, 0, 0, :], in_=gains[:, :, 0, :])
+            nc.scalar.mul(out=wsg[:, :, 0, 1, :], in_=gains[:, :, 1, :], mul=-1.0)
 
         tab = const.tile([P, A, 2, 2, HD], F32)
 
@@ -386,13 +384,13 @@ def tile_qwen3block_pa_t_kernel(tc, x, ln_w, qkv_w, q_norm_w, k_norm_w, out_0, o
             if 0 <= i < NT:
                 stage(i)
 
+        stage_square(0)
+        stage_square(1)
         reduce_angles(0, FIRST_ANGLES)
         sines(0, FIRST_ANGLES)
-        for i in range(EARLY):
-            stage_square(i)
         reduce_angles(FIRST_ANGLES, A)
-        sines(FIRST_ANGLES, A)
         spread_rows()
+        sines(FIRST_ANGLES, A)
         for i in range(0, EARLY, 2):
             early_rsqrt(i, 2)
         pieces = [(blk, piece) for blk in range(A // TABLE_BLOCK) for piece in range(3)]

@@ -112,6 +112,8 @@ def tile_qwen3block_pa_t_kernel(tc, x, ln_w, qkv_w, q_norm_w, k_norm_w, out_0, o
 
         ones_b = const.tile([P, P], BF16)
         nc.vector.memset(ones_b[:], 1.0)
+        minus_b = const.tile([P, P], BF16)
+        nc.vector.memset(minus_b[:], -1.0)
         one1 = const.tile([P, 1], F32)
         nc.vector.memset(one1[:], 1.0)
         eps_t = const.tile([P, 1], F32)
@@ -184,29 +186,34 @@ def tile_qwen3block_pa_t_kernel(tc, x, ln_w, qkv_w, q_norm_w, k_norm_w, out_0, o
             nc.scalar.activation(out=cs[:, a0:a1, 1, :], in_=fr[:, a0:a1, :], func=ACT.Sin, scale=2.0 * math.pi)
 
         lnw_bc = ps_c.tile([P, E], F32)
-        wsg = const.tile([P, 2, 2, 2, PAIRS], F32)
+        wsg = const.tile([P, 2, 2, HD], F32)
+        pskv = ps_kv.tile([P, BANK], F32)
+        gains = pskv[:].rearrange("p (e q d) -> p e q d", e=2, q=2)
 
         def spread_rows():
             nc.tensor.matmul(out=lnw_bc[:], lhsT=ones_b[:], rhs=rows[:, 0:E], start=True, stop=True)
-            xT = ps_t.tile([P, PACK, P], F32)
+            w_row = rows[:, E : E + 2 * HD].rearrange("p (q j f) -> p q f j", q=2, f=2)
             nc.tensor.matmul(
-                out=xT[:, 0:2, :].rearrange("p a b -> p (a b)"), lhsT=ones_b[:], rhs=rows[:, E : E + 2 * HD],
+                out=gains[:, 1, :, :].rearrange("p q (f j) -> p q f j", f=2), lhsT=ones_b[:], rhs=w_row,
                 start=True, stop=True,
             )
-            gains = xT[:, 0:2, :].rearrange("p q (j f) -> p q f j", f=2)
-            nc.scalar.copy(out=wsg[:, :, 1, :, :], in_=gains)
-            nc.scalar.copy(out=wsg[:, :, 0, 0, :], in_=gains[:, :, 0, :])
-            nc.scalar.mul(out=wsg[:, :, 0, 1, :], in_=gains[:, :, 1, :], mul=-1.0)
+            for f, sign in enumerate((ones_b, minus_b)):
+                nc.tensor.matmul(
+                    out=gains[:, 0, :, PAIRS * f : PAIRS * f + PAIRS], lhsT=sign[:], rhs=w_row[:, :, f, :],
+                    start=True, stop=True,
+                )
+            nc.scalar.copy(out=wsg[:].rearrange("p e q d -> p (e q d)"), in_=pskv[:])
 
         tab = const.tile([P, A, 2, 2, HD], F32)
 
         def table_piece(blk, piece, eng):
             a = slice(TABLE_BLOCK * blk, TABLE_BLOCK * (blk + 1))
+            w = gains if blk < VECTOR_TABLES else wsg
             if piece == 0:
                 eng.tensor_tensor(
                     out=tab[:, a, :, 0, :],
                     in0=cs[:, a, :, :].rearrange("p a c j -> p a (c j)").unsqueeze(2).to_broadcast([P, TABLE_BLOCK, 2, HD]),
-                    in1=wsg[:, :, 0, :, :].rearrange("p q f j -> p q (f j)").unsqueeze(1).to_broadcast([P, TABLE_BLOCK, 2, HD]),
+                    in1=w[:, 0, :, :].unsqueeze(1).to_broadcast([P, TABLE_BLOCK, 2, HD]),
                     op=ALU.mult,
                 )
             else:
@@ -214,7 +221,7 @@ def tile_qwen3block_pa_t_kernel(tc, x, ln_w, qkv_w, q_norm_w, k_norm_w, out_0, o
                 eng.tensor_tensor(
                     out=tab[:, a, :, 1, PAIRS * f : PAIRS * f + PAIRS],
                     in0=cs[:, a, 1 - f, :].unsqueeze(2).to_broadcast([P, TABLE_BLOCK, 2, PAIRS]),
-                    in1=wsg[:, :, 1, f, :].unsqueeze(1).to_broadcast([P, TABLE_BLOCK, 2, PAIRS]),
+                    in1=w[:, 1, :, PAIRS * f : PAIRS * f + PAIRS].unsqueeze(1).to_broadcast([P, TABLE_BLOCK, 2, PAIRS]),
                     op=ALU.mult,
                 )
 

@@ -46,8 +46,11 @@ TABLES_AT_START = 3
 TABLE_BLOCK = 4
 FIRST_ANGLES = 4
 HEAD_ORDER = (4, 5, 0, 1, 2, 3)
-QUANT_AFTER = 5
+QUANT_AFTER = 6
 VECTOR_TABLES = 1
+PIECE_FROM = 5
+PIECE_EVERY = 1
+VSUM = NT - 2
 
 
 def quant_batches():
@@ -94,7 +97,7 @@ def tile_qwen3block_pa_t_kernel(tc, x, ln_w, qkv_w, q_norm_w, k_norm_w, out_0, o
         batches = quant_batches()
 
         rows = const.tile([P, E + 2 * HD], BF16)
-        nc.gpsimd.memset(rows[:], 0.0)
+        nc.gpsimd.memset(rows[:].bitcast(U32), 0)
 
         xin = {}
         wr = const.tile([P, PACK, F], BF16)
@@ -110,12 +113,10 @@ def tile_qwen3block_pa_t_kernel(tc, x, ln_w, qkv_w, q_norm_w, k_norm_w, out_0, o
             if g == 1:
                 nc.sync.dma_start(out=wr[:], in_=qkv_w.rearrange("(p t) n -> p t n", t=PACK))
 
-        ones_b = const.tile([P, P], BF16)
-        nc.vector.memset(ones_b[:], 1.0)
-        minus_b = const.tile([P, P], BF16)
-        nc.vector.memset(minus_b[:], -1.0)
         one1 = const.tile([P, 1], F32)
         nc.vector.memset(one1[:], 1.0)
+        ones_b = const.tile([P, P], BF16)
+        minus_b = const.tile([P, P], BF16)
         eps_t = const.tile([P, 1], F32)
         nc.vector.memset(eps_t[:], EPS)
         pos_i = const.tile([P, A], I32)
@@ -136,6 +137,8 @@ def tile_qwen3block_pa_t_kernel(tc, x, ln_w, qkv_w, q_norm_w, k_norm_w, out_0, o
                     out=gt[:, width * m : width * m + width], in0=gt[:, 0:width],
                     scalar1=ROPE_BASE ** (-width * m / 64.0),
                 )
+        nc.vector.memset(ones_b[:], 1.0)
+        nc.vector.memset(minus_b[:], -1.0)
         pos_f = const.tile([P, A], F32)
         nc.vector.tensor_copy(out=pos_f[:], in_=pos_i[:])
         halfpi = const.tile([P, 1], F32)
@@ -355,7 +358,7 @@ def tile_qwen3block_pa_t_kernel(tc, x, ln_w, qkv_w, q_norm_w, k_norm_w, out_0, o
         def stage_sum(i):
             ap, b, u = tile_coords(i)
             o_t = st[("o", i // 2)]
-            sum_heads(i, 0, NH, nc.gpsimd)
+            sum_heads(i, 0, NH, nc.vector if i >= VSUM else nc.gpsimd)
             if i >= NT - 2:
                 us, sl = slice(u, u + 1), slice(2 * ap + u, 2 * ap + u + 1)
             elif u == 1:
@@ -382,6 +385,8 @@ def tile_qwen3block_pa_t_kernel(tc, x, ln_w, qkv_w, q_norm_w, k_norm_w, out_0, o
 
             stage_rotate(i, 0, 2)
             stage_rotate(i, 2, 4)
+            if VSUM < i:
+                stage_sum(i - 1)
             add_and_store(HEAD_ORDER[0])
             stage_rotate(i, 4, 6)
             add_and_store(HEAD_ORDER[2])
@@ -402,11 +407,11 @@ def tile_qwen3block_pa_t_kernel(tc, x, ln_w, qkv_w, q_norm_w, k_norm_w, out_0, o
             early_rsqrt(i, 2)
         pieces = [(blk, piece) for blk in range(A // TABLE_BLOCK) for piece in range(3)]
         vector_pieces = pieces[: 3 * VECTOR_TABLES]
+        weights()
         for ap, piece in pieces[3 * VECTOR_TABLES : 3 * TABLES_AT_START]:
             table_piece(ap, piece, nc.gpsimd)
         later_pieces = pieces[3 * TABLES_AT_START :]
 
-        weights()
         slots = NT + LAG_QUANT + 1
         written = 0
         pending = []
@@ -415,8 +420,9 @@ def tile_qwen3block_pa_t_kernel(tc, x, ln_w, qkv_w, q_norm_w, k_norm_w, out_0, o
             written = max(written, min(slots, slots_by_step(step)))
             on(stage_matmul, step - LAG_MATMUL)
             if step - LAG_SUM < NT - 1:
-                on(stage_sum, step - LAG_SUM)
-            if step > LAG_SUM and later_pieces:
+                if step - LAG_SUM < VSUM:
+                    on(stage_sum, step - LAG_SUM)
+            if step >= PIECE_FROM and (step - PIECE_FROM) % PIECE_EVERY == 0 and later_pieces:
                 table_piece(*later_pieces.pop(0), nc.gpsimd)
             on(stage_headnorm, step - LAG_HEADNORM)
             if step - LAG_ROTATE == NT - 1:

@@ -48,9 +48,10 @@ FIRST_ANGLES = 4
 HEAD_ORDER = (4, 5, 0, 1, 2, 3)
 QUANT_AFTER = 6
 VECTOR_TABLES = 1
+SINGLE = 4
 PIECE_FROM = 5
-PIECE_EVERY = 1
-VSUM = NT - 2
+PIECE_EVERY = 4
+VSUM = NT - 1
 
 
 def quant_batches():
@@ -144,25 +145,29 @@ def tile_qwen3block_pa_t_kernel(tc, x, ln_w, qkv_w, q_norm_w, k_norm_w, out_0, o
         halfpi = const.tile([P, 1], F32)
         nc.vector.tensor_scalar_mul(out=halfpi[:], in0=one1[:], scalar1=math.pi / 2.0)
 
-        ssx = const.tile([P, NT], F32)
-        rx = const.tile([P, NT], F32)
+        both_pool = ctx.enter_context(tc.tile_pool(name="both_pool", bufs=6))
 
         def stage_square(i):
             xt = xin[i // 2][:, i % 2, :]
             junk_x = j_pool.tile([P, E], BF16)
-            nc.scalar.activation(out=junk_x[:], in_=xt, func=ACT.Square, accum_out=ssx[:, i : i + 1])
+            if i % 2 == 0:
+                both = both_pool.tile([P, NH + 2], F32)
+                st[("sums", i)] = both
+            sums = st[("sums", i - i % 2)]
+            nc.scalar.activation(
+                out=junk_x[:], in_=xt, func=ACT.Square, scale=E ** -0.5, accum_out=sums[:, NH + i % 2 : NH + i % 2 + 1]
+            )
 
         def stage_rsqrt(i):
-            nc.scalar.activation(
-                out=rx[:, i : i + 2], in_=ssx[:, i : i + 2], func=ACT.Abs_reciprocal_sqrt,
-                scale=1.0 / E, bias=eps_t[:],
-            )
+            early_rsqrt(i, 2)
 
         def early_rsqrt(i, n):
-            cols = slice(i, i + n)
+            rx = both_pool.tile([P, 2], F32)
             nc.scalar.activation(
-                out=rx[:, cols], in_=ssx[:, cols], func=ACT.Abs_reciprocal_sqrt, scale=1.0 / E, bias=eps_t[:]
+                out=rx[:], in_=st[("sums", i)][:, NH : NH + 2], func=ACT.Abs_reciprocal_sqrt, bias=eps_t[:]
             )
+            st[("rx", i)] = rx[:, 0:1]
+            st[("rx", i + 1)] = rx[:, 1:2]
 
         tt = const.tile([P, A, PAIRS], F32)
         n_s = const.tile([P, A, PAIRS], I32)
@@ -183,10 +188,10 @@ def tile_qwen3block_pa_t_kernel(tc, x, ln_w, qkv_w, q_norm_w, k_norm_w, out_0, o
 
         def sines(a0, a1):
             nc.scalar.activation(out=af[:, a0:a1, :], in_=fr[:, a0:a1, :], func=ACT.Abs)
+            nc.scalar.activation(out=cs[:, a0:a1, 1, :], in_=fr[:, a0:a1, :], func=ACT.Sin, scale=2.0 * math.pi)
             nc.scalar.activation(
                 out=cs[:, a0:a1, 0, :], in_=af[:, a0:a1, :], func=ACT.Sin, scale=-2.0 * math.pi, bias=halfpi[:]
             )
-            nc.scalar.activation(out=cs[:, a0:a1, 1, :], in_=fr[:, a0:a1, :], func=ACT.Sin, scale=2.0 * math.pi)
 
         lnw_bc = ps_c.tile([P, E], F32)
         wsg = const.tile([P, 2, 2, HD], F32)
@@ -249,7 +254,7 @@ def tile_qwen3block_pa_t_kernel(tc, x, ln_w, qkv_w, q_norm_w, k_norm_w, out_0, o
             xt = xin[i // 2][:, i % 2, :]
             xs = xs_pool.tile([P, E], BF16)
             nc.vector.scalar_tensor_tensor(
-                out=xs[:], in0=xt, scalar=rx[:, i : i + 1], in1=lnw_bc[:], op0=ALU.mult, op1=ALU.mult
+                out=xs[:], in0=xt, scalar=st[("rx", i)], in1=lnw_bc[:], op0=ALU.mult, op1=ALU.mult
             )
             st[("xs", i)] = xs
 
@@ -305,26 +310,34 @@ def tile_qwen3block_pa_t_kernel(tc, x, ln_w, qkv_w, q_norm_w, k_norm_w, out_0, o
                 return psq[:, HD * h : HD * h + HD]
             return pskv[:, HD * (h - NQ) : HD * (h - NQ) + HD]
 
-        def stage_headnorm(i):
+        def stage_headnorm(i, pair):
             u = i % 2
             if u == 0:
                 o_t = o_pool.tile([P, 2, F], F32)
                 st[("o", i // 2)] = o_t
             o_t = st[("o", i // 2)]
-            ssh = small.tile([P, NH], F32)
+            if pair is None:
+                ssh = small.tile([P, NH], F32)
+                width = NH
+            else:
+                ssh = st[("sums", pair)]
+                width = NH + 2
             junk_h = j_pool.tile([P, NH, HD], BF16)
             for h in range(NH):
                 nc.scalar.activation(
-                    out=junk_h[:, h, :], in_=head_cols(i, h), func=ACT.Square, accum_out=ssh[:, h : h + 1]
+                    out=junk_h[:, h, :], in_=head_cols(i, h), func=ACT.Square, scale=HD ** -0.5, accum_out=ssh[:, h : h + 1]
                 )
             nc.scalar.copy(out=o_t[:, u, QK:F], in_=st[("ps", i)][1][:, BANK - (F - QK) : BANK])
-            if i >= NT - 2:
+            if i >= NT - SINGLE:
                 ap, b, u = tile_coords(i)
                 nc.sync.dma_start(out=o2v[b, :, 2 * ap + u : 2 * ap + u + 1, :], in_=o_t[:, u : u + 1, QK:F])
-            rh = small.tile([P, NH], F32)
+            rh = both_pool.tile([P, NH + 2], F32)
             nc.scalar.activation(
-                out=rh[:], in_=ssh[:], func=ACT.Abs_reciprocal_sqrt, scale=1.0 / HD, bias=eps_t[:]
+                out=rh[:, 0:width], in_=ssh[:, 0:width], func=ACT.Abs_reciprocal_sqrt, bias=eps_t[:]
             )
+            if pair is not None:
+                st[("rx", pair)] = rh[:, NH : NH + 1]
+                st[("rx", pair + 1)] = rh[:, NH + 1 : NH + 2]
             st[("rh", i)] = rh
 
         def stage_rotate(i, h0, h1):
@@ -358,16 +371,20 @@ def tile_qwen3block_pa_t_kernel(tc, x, ln_w, qkv_w, q_norm_w, k_norm_w, out_0, o
         def stage_sum(i):
             ap, b, u = tile_coords(i)
             o_t = st[("o", i // 2)]
-            sum_heads(i, 0, NH, nc.vector if i >= VSUM else nc.gpsimd)
-            if i >= NT - 2:
+            if i == NT - 2:
+                sum_heads(i, 0, NQ, nc.gpsimd)
+            else:
+                sum_heads(i, 0, NH, nc.gpsimd)
+            if i >= NT - SINGLE:
                 us, sl = slice(u, u + 1), slice(2 * ap + u, 2 * ap + u + 1)
             elif u == 1:
                 us, sl = slice(0, 2), slice(2 * ap, 2 * ap + 2)
             else:
                 return
             nc.sync.dma_start(out=o0v[b, :, sl, :], in_=o_t[:, us, 0 : NQ * HD])
-            nc.sync.dma_start(out=o1v[b, :, sl, :], in_=o_t[:, us, NQ * HD : QK])
-            if i < NT - 2:
+            if i != NT - 2:
+                nc.sync.dma_start(out=o1v[b, :, sl, :], in_=o_t[:, us, NQ * HD : QK])
+            if i < NT - SINGLE:
                 nc.sync.dma_start(out=o2v[b, :, sl, :], in_=o_t[:, us, QK:F])
 
         def last_tile():
@@ -385,8 +402,8 @@ def tile_qwen3block_pa_t_kernel(tc, x, ln_w, qkv_w, q_norm_w, k_norm_w, out_0, o
 
             stage_rotate(i, 0, 2)
             stage_rotate(i, 2, 4)
-            if VSUM < i:
-                stage_sum(i - 1)
+            sum_heads(i - 1, NQ, NH, nc.vector)
+            nc.sync.dma_start(out=o1v[b, :, 2 * ap : 2 * ap + 1, :], in_=o_t[:, 0:1, NQ * HD : QK])
             add_and_store(HEAD_ORDER[0])
             stage_rotate(i, 4, 6)
             add_and_store(HEAD_ORDER[2])
@@ -408,10 +425,14 @@ def tile_qwen3block_pa_t_kernel(tc, x, ln_w, qkv_w, q_norm_w, k_norm_w, out_0, o
         pieces = [(blk, piece) for blk in range(A // TABLE_BLOCK) for piece in range(3)]
         vector_pieces = pieces[: 3 * VECTOR_TABLES]
         weights()
+        gate = const.tile([P, 1], U32)
+        nc.gpsimd.tensor_copy(out=gate[:], in_=wc[:, F - 1 : F])
         for ap, piece in pieces[3 * VECTOR_TABLES : 3 * TABLES_AT_START]:
             table_piece(ap, piece, nc.gpsimd)
         later_pieces = pieces[3 * TABLES_AT_START :]
 
+        for blk, piece in vector_pieces[:1]:
+            table_piece(blk, piece, nc.vector)
         slots = NT + LAG_QUANT + 1
         written = 0
         pending = []
@@ -424,7 +445,11 @@ def tile_qwen3block_pa_t_kernel(tc, x, ln_w, qkv_w, q_norm_w, k_norm_w, out_0, o
                     on(stage_sum, step - LAG_SUM)
             if step >= PIECE_FROM and (step - PIECE_FROM) % PIECE_EVERY == 0 and later_pieces:
                 table_piece(*later_pieces.pop(0), nc.gpsimd)
-            on(stage_headnorm, step - LAG_HEADNORM)
+            merged = None
+            if len(due) == 1 and due[0] % 2 == 0 and due[0] - LAG_RSQRT < NT and 0 <= step - LAG_HEADNORM < NT:
+                merged = due[0] - LAG_RSQRT
+            if 0 <= step - LAG_HEADNORM < NT:
+                stage_headnorm(step - LAG_HEADNORM, merged)
             if step - LAG_ROTATE == NT - 1:
                 last_tile()
             if 0 <= step - LAG_ROTATE < NT - 1:
@@ -437,7 +462,7 @@ def tile_qwen3block_pa_t_kernel(tc, x, ln_w, qkv_w, q_norm_w, k_norm_w, out_0, o
             for s in due:
                 if s >= EARLY:
                     on(stage_square, s)
-                if s - LAG_RSQRT >= EARLY and s % 2 == 0:
+                if s - LAG_RSQRT >= EARLY and s % 2 == 0 and merged is None:
                     on(stage_rsqrt, s - LAG_RSQRT)
                 on(stage_scale, s - LAG_SCALE)
                 if s % 2 == 1:
@@ -451,5 +476,6 @@ def tile_qwen3block_pa_t_kernel(tc, x, ln_w, qkv_w, q_norm_w, k_norm_w, out_0, o
                         stage_quantise(batches[i][0], batches[i][2])
                     else:
                         pending.append((batches[i][0], batches[i][2]))
-            for ap, piece in vector_pieces[3 * step : 3 * step + 3]:
-                table_piece(ap, piece, nc.vector)
+            if step == 0:
+                for blk, piece in vector_pieces[1:]:
+                    table_piece(blk, piece, nc.vector)

@@ -48,7 +48,7 @@ FIRST_ANGLES = 4
 HEAD_ORDER = (4, 5, 0, 1, 2, 3)
 QUANT_AFTER = 6
 VECTOR_TABLES = 1
-SINGLE = 4
+SINGLE = 6
 PIECE_FROM = 5
 PIECE_EVERY = 4
 VSUM = NT - 1
@@ -111,7 +111,7 @@ def tile_qwen3block_pa_t_kernel(tc, x, ln_w, qkv_w, q_norm_w, k_norm_w, out_0, o
                 nc.sync.dma_start(out=rows[0:1, 0:E], in_=ln_w.rearrange("(o k) -> o k", o=1))
                 nc.sync.dma_start(out=rows[0:1, E : E + HD], in_=q_norm_w.rearrange("(o k) -> o k", o=1))
                 nc.sync.dma_start(out=rows[0:1, E + HD : E + 2 * HD], in_=k_norm_w.rearrange("(o k) -> o k", o=1))
-            if g == 1:
+            if g == 0:
                 nc.sync.dma_start(out=wr[:], in_=qkv_w.rearrange("(p t) n -> p t n", t=PACK))
 
         one1 = const.tile([P, 1], F32)
@@ -132,14 +132,15 @@ def tile_qwen3block_pa_t_kernel(tc, x, ln_w, qkv_w, q_norm_w, k_norm_w, out_0, o
             nc.vector.tensor_scalar_mul(
                 out=gt[:, j : j + 1], in0=one1[:], scalar1=ROPE_BASE ** (-j / 64.0) / (2.0 * math.pi)
             )
+        fillers = [ones_b, minus_b]
         for width in (4, 16):
+            nc.vector.memset(fillers[0][:], 1.0 if width == 4 else -1.0)
+            fillers.pop(0)
             for m in range(1, 4):
                 nc.vector.tensor_scalar_mul(
                     out=gt[:, width * m : width * m + width], in0=gt[:, 0:width],
                     scalar1=ROPE_BASE ** (-width * m / 64.0),
                 )
-        nc.vector.memset(ones_b[:], 1.0)
-        nc.vector.memset(minus_b[:], -1.0)
         pos_f = const.tile([P, A], F32)
         nc.vector.tensor_copy(out=pos_f[:], in_=pos_i[:])
         halfpi = const.tile([P, 1], F32)
@@ -273,9 +274,8 @@ def tile_qwen3block_pa_t_kernel(tc, x, ln_w, qkv_w, q_norm_w, k_norm_w, out_0, o
                 hg = h_pool.tile([P, nb, P, PACK], BF16, align_bytes=64)
                 st[("hg", qb)] = hg
             hg = st[("hg", qb)]
-            nc.scalar.copy(
-                out=hg[:, i - first : i - first + 2, :, :].bitcast(F32), in_=xT[:].rearrange("p n u r -> p n r u")
-            )
+            copy = nc.vector.tensor_copy if i == 0 else nc.scalar.copy
+            copy(out=hg[:, i - first : i - first + 2, :, :].bitcast(F32), in_=xT[:].rearrange("p n u r -> p n r u"))
 
         def stage_quantise(qb, nb):
             hg = st[("hg", qb)]

import math
from contextlib import ExitStack

import concourse.mybir as mybir
from concourse.masks import make_identity

FLOPS = 2 * 4096 * 512 * 1024

F32 = mybir.dt.float32
BF16 = mybir.dt.bfloat16
I32 = mybir.dt.int32
U32 = mybir.dt.uint32
U8 = mybir.dt.uint8
FP8X4 = mybir.dt.float8_e4m3fn_x4
ALU = mybir.AluOpType
ACT = mybir.ActivationFunctionType

P = 128
PACK = 4
E = P * PACK
A = 16
NT = 2 * A
HD = 128
PAIRS = HD // 2
NQ = 4
NH = 6
QK = NH * HD
F = 1024
BANK = 512
EPS = 1e-6
ROPE_BASE = 1000000.0

QUANT_BATCH = (2, 2, 4, 4, 4, 4, 4, 4, 4)
EARLY = 2
LAG_RSQRT = 2
LAG_SCALE = 3
LAG_TRANSPOSE = 5
LAG_ROUND = 6
LAG_QUANT = 6
LAG_MATMUL = 1
LAG_HEADNORM = 2
LAG_ROTATE = 3
LAG_SUM = 4
LEAD = LAG_QUANT + max(QUANT_BATCH) + 1
TABLES_AT_START = 3
TABLE_BLOCK = 4
FIRST_ANGLES = 4
HEAD_ORDER = (4, 5, 0, 1, 2, 3)
QUANT_AFTER = 6
VECTOR_TABLES = 1
SINGLE = 6
PIECE_FROM = 5
PIECE_EVERY = 4
VSUM = NT - 1


def quant_batches():
    first, table = 0, {}
    for qb, nb in enumerate(QUANT_BATCH):
        for i in range(first, first + nb):
            table[i] = (qb, first, nb)
        first += nb
    assert first == NT
    return table


def slots_by_step(step):
    return min(LAG_QUANT + 2 + 2 * step, step + LEAD)


def tile_qwen3block_pa_t_kernel(tc, x, ln_w, qkv_w, q_norm_w, k_norm_w, out_0, out_1, out_2):
    nc = tc.nc
    with ExitStack() as ctx:
        const = ctx.enter_context(tc.tile_pool(name="const", bufs=1))
        small = ctx.enter_context(tc.tile_pool(name="small", bufs=4))
        xs_pool = ctx.enter_context(tc.tile_pool(name="xs_pool", bufs=4))
        h_pool = ctx.enter_context(tc.tile_pool(name="h_pool", bufs=3))
        c_pool = ctx.enter_context(tc.tile_pool(name="c_pool", bufs=3))
        j_pool = ctx.enter_context(tc.tile_pool(name="j_pool", bufs=3))
        t_pool = ctx.enter_context(tc.tile_pool(name="t_pool", bufs=5))
        o_pool = ctx.enter_context(tc.tile_pool(name="o_pool", bufs=4))
        ps_t = ctx.enter_context(tc.psum_pool(name="ps_t", bufs=2))
        ps_c = ctx.enter_context(tc.psum_pool(name="ps_c", bufs=1))
        ps_mx = ctx.enter_context(tc.psum_pool(name="ps_mx", bufs=3))
        ps_kv = ctx.enter_context(tc.psum_pool(name="ps_kv", bufs=2))
        ctx.enter_context(tc.manual_schedule())

        xv = x.rearrange("b (p a) e -> b p a e", a=A)
        o0v = out_0.rearrange("b (p a) h d -> b p a (h d)", a=A)
        o1v = out_1.rearrange("b (p a) h d -> b p a (h d)", a=A)
        o2v = out_2.rearrange("b (p a) h d -> b p a (h d)", a=A)

        def tile_coords(i):
            g = i // 2
            return g // 2, g % 2, i % 2

        st = {}
        batches = quant_batches()

        rows = const.tile([P, E + 2 * HD], BF16)
        nc.gpsimd.memset(rows[:].bitcast(U32), 0)

        xin = {}
        wr = const.tile([P, PACK, F], BF16)
        for g in range(NT // 2):
            ap, b = g // 2, g % 2
            xg = const.tile([P, 2, E], BF16, name="xg%d" % g)
            nc.sync.dma_start(out=xg[:], in_=xv[b, :, 2 * ap : 2 * ap + 2, :])
            xin[g] = xg
            if g == 0:
                nc.sync.dma_start(out=rows[0:1, 0:E], in_=ln_w.rearrange("(o k) -> o k", o=1))
                nc.sync.dma_start(out=rows[0:1, E : E + HD], in_=q_norm_w.rearrange("(o k) -> o k", o=1))
                nc.sync.dma_start(out=rows[0:1, E + HD : E + 2 * HD], in_=k_norm_w.rearrange("(o k) -> o k", o=1))
            if g == 0:
                nc.sync.dma_start(out=wr[:], in_=qkv_w.rearrange("(p t) n -> p t n", t=PACK))

        one1 = const.tile([P, 1], F32)
        nc.vector.memset(one1[:], 1.0)
        ones_b = const.tile([P, P], BF16)
        minus_b = const.tile([P, P], BF16)
        eps_t = const.tile([P, 1], F32)
        nc.vector.memset(eps_t[:], EPS)
        pos_i = const.tile([P, A], I32)
        nc.gpsimd.iota(pos_i[:], pattern=[[1, A]], base=0, channel_multiplier=A)
        identf = const.tile([P, P], F32)
        make_identity(nc, identf[:])
        junk1 = const.tile([P, 1], F32)
        nc.scalar.activation(out=junk1[:], in_=one1[:], func=ACT.Sin)

        gt = const.tile([P, PAIRS], F32)
        for j in range(4):
            nc.vector.tensor_scalar_mul(
                out=gt[:, j : j + 1], in0=one1[:], scalar1=ROPE_BASE ** (-j / 64.0) / (2.0 * math.pi)
            )
        fillers = [ones_b, minus_b]
        for width in (4, 16):
            nc.vector.memset(fillers[0][:], 1.0 if width == 4 else -1.0)
            fillers.pop(0)
            for m in range(1, 4):
                nc.vector.tensor_scalar_mul(
                    out=gt[:, width * m : width * m + width], in0=gt[:, 0:width],
                    scalar1=ROPE_BASE ** (-width * m / 64.0),
                )
        pos_f = const.tile([P, A], F32)
        nc.vector.tensor_copy(out=pos_f[:], in_=pos_i[:])
        halfpi = const.tile([P, 1], F32)
        nc.vector.tensor_scalar_mul(out=halfpi[:], in0=one1[:], scalar1=math.pi / 2.0)

        both_pool = ctx.enter_context(tc.tile_pool(name="both_pool", bufs=6))

        def stage_square(i):
            xt = xin[i // 2][:, i % 2, :]
            junk_x = j_pool.tile([P, E], BF16)
            if i % 2 == 0:
                both = both_pool.tile([P, NH + 2], F32)
                st[("sums", i)] = both
            sums = st[("sums", i - i % 2)]
            nc.scalar.activation(
                out=junk_x[:], in_=xt, func=ACT.Square, scale=E ** -0.5, accum_out=sums[:, NH + i % 2 : NH + i % 2 + 1]
            )

        def stage_rsqrt(i):
            early_rsqrt(i, 2)

        def early_rsqrt(i, n):
            rx = both_pool.tile([P, 2], F32)
            nc.scalar.activation(
                out=rx[:], in_=st[("sums", i)][:, NH : NH + 2], func=ACT.Abs_reciprocal_sqrt, bias=eps_t[:]
            )
            st[("rx", i)] = rx[:, 0:1]
            st[("rx", i + 1)] = rx[:, 1:2]

        tt = const.tile([P, A, PAIRS], F32)
        n_s = const.tile([P, A, PAIRS], I32)
        fr = const.tile([P, A, PAIRS], F32)
        af = const.tile([P, A, PAIRS], F32)
        cs = const.tile([P, A, 2, PAIRS], F32)

        def reduce_angles(a0, a1):
            na = a1 - a0
            nc.vector.tensor_tensor(
                out=tt[:, a0:a1, :],
                in0=pos_f[:, a0:a1].unsqueeze(2).to_broadcast([P, na, PAIRS]),
                in1=gt[:].unsqueeze(1).to_broadcast([P, na, PAIRS]),
                op=ALU.mult,
            )
            nc.vector.tensor_copy(out=n_s[:, a0:a1, :], in_=tt[:, a0:a1, :])
            nc.vector.tensor_tensor(out=fr[:, a0:a1, :], in0=tt[:, a0:a1, :], in1=n_s[:, a0:a1, :], op=ALU.subtract)

        def sines(a0, a1):
            nc.scalar.activation(out=af[:, a0:a1, :], in_=fr[:, a0:a1, :], func=ACT.Abs)
            nc.scalar.activation(out=cs[:, a0:a1, 1, :], in_=fr[:, a0:a1, :], func=ACT.Sin, scale=2.0 * math.pi)
            nc.scalar.activation(
                out=cs[:, a0:a1, 0, :], in_=af[:, a0:a1, :], func=ACT.Sin, scale=-2.0 * math.pi, bias=halfpi[:]
            )

        lnw_bc = ps_c.tile([P, E], F32)
        wsg = const.tile([P, 2, 2, HD], F32)
        pskv = ps_kv.tile([P, BANK], F32)
        gains = pskv[:].rearrange("p (e q d) -> p e q d", e=2, q=2)

        def spread_rows():
            nc.tensor.matmul(out=lnw_bc[:], lhsT=ones_b[:], rhs=rows[:, 0:E], start=True, stop=True)
            w_row = rows[:, E : E + 2 * HD].rearrange("p (q j f) -> p q f j", q=2, f=2)
            nc.tensor.matmul(
                out=gains[:, 1, :, :].rearrange("p q (f j) -> p q f j", f=2), lhsT=ones_b[:], rhs=w_row,
                start=True, stop=True,
            )
            for f, sign in enumerate((ones_b, minus_b)):
                nc.tensor.matmul(
                    out=gains[:, 0, :, PAIRS * f : PAIRS * f + PAIRS], lhsT=sign[:], rhs=w_row[:, :, f, :],
                    start=True, stop=True,
                )
            nc.scalar.copy(out=wsg[:].rearrange("p e q d -> p (e q d)"), in_=pskv[:])

        tab = const.tile([P, A, 2, 2, HD], F32)

        def table_piece(blk, piece, eng):
            a = slice(TABLE_BLOCK * blk, TABLE_BLOCK * (blk + 1))
            w = gains if blk < VECTOR_TABLES else wsg
            if piece == 0:
                eng.tensor_tensor(
                    out=tab[:, a, :, 0, :],
                    in0=cs[:, a, :, :].rearrange("p a c j -> p a (c j)").unsqueeze(2).to_broadcast([P, TABLE_BLOCK, 2, HD]),
                    in1=w[:, 0, :, :].unsqueeze(1).to_broadcast([P, TABLE_BLOCK, 2, HD]),
                    op=ALU.mult,
                )
            else:
                f = piece - 1
                eng.tensor_tensor(
                    out=tab[:, a, :, 1, PAIRS * f : PAIRS * f + PAIRS],
                    in0=cs[:, a, 1 - f, :].unsqueeze(2).to_broadcast([P, TABLE_BLOCK, 2, PAIRS]),
                    in1=w[:, 1, :, PAIRS * f : PAIRS * f + PAIRS].unsqueeze(1).to_broadcast([P, TABLE_BLOCK, 2, PAIRS]),
                    op=ALU.mult,
                )

        wg = const.tile([P, F, PACK], BF16, align_bytes=64)
        wc = const.tile([P, F], U32, align_bytes=64)
        ws = const.tile([P, F], U8, align_bytes=64)

        def weights():
            wg_qk = wg[:, 0:QK, :].rearrange("p (h f j) t -> p f h j t", f=2, j=PAIRS)
            wr_qk = wr[:, :, 0:QK].rearrange("p t (h j f) -> p f h j t", f=2, j=PAIRS)
            for f in range(2):
                nc.vector.tensor_copy(out=wg_qk[:, f, :, :, :], in_=wr_qk[:, f, :, :, :])
            nc.vector.tensor_copy(out=wg[:, QK:F, :], in_=wr[:, :, QK:F].rearrange("p t n -> p n t"))
            for c in range(2):
                nc.vector.quantize_mx(
                    out=wc[:, BANK * c : BANK * c + BANK].bitcast(FP8X4),
                    scales=ws[:, BANK * c : BANK * c + BANK],
                    in_=wg[:, BANK * c : BANK * c + BANK, :].rearrange("p n t -> p (n t)"),
                )

        def stage_scale(i):
            xt = xin[i // 2][:, i % 2, :]
            xs = xs_pool.tile([P, E], BF16)
            nc.vector.scalar_tensor_tensor(
                out=xs[:], in0=xt, scalar=st[("rx", i)], in1=lnw_bc[:], op0=ALU.mult, op1=ALU.mult
            )
            st[("xs", i)] = xs

        def stage_transpose(i):
            xT = ps_t.tile([P, 2, 2, P], F32)
            for n in range(2):
                words = st[("xs", i + n)][:].bitcast(F32)
                for u in range(2):
                    nc.tensor.transpose(out=xT[:, n, u, :], in_=words[:, u : E // 2 : 2], identity=identf[:])
            st[("xT", i)] = xT

        def stage_round(i):
            xT = st[("xT", i)]
            qb, first, nb = batches[i]
            if i == first:
                hg = h_pool.tile([P, nb, P, PACK], BF16, align_bytes=64)
                st[("hg", qb)] = hg
            hg = st[("hg", qb)]
            copy = nc.vector.tensor_copy if i == 0 else nc.scalar.copy
            copy(out=hg[:, i - first : i - first + 2, :, :].bitcast(F32), in_=xT[:].rearrange("p n u r -> p n r u"))

        def stage_quantise(qb, nb):
            hg = st[("hg", qb)]
            hc = c_pool.tile([P, nb * P], U32, align_bytes=64)
            hs = c_pool.tile([P, nb * P], U8, align_bytes=64)
            nc.vector.quantize_mx(
                out=hc[:].bitcast(FP8X4), scales=hs[:], in_=hg[:].rearrange("p n r t -> p (n r t)")
            )
            st[("hc", qb)] = (hc, hs)

        def stage_matmul(i):
            qb, first, nb = batches[i]
            hc, hs = st[("hc", qb)]
            cols = slice(P * (i - first), P * (i - first) + P)
            psq = ps_mx.tile([P, BANK], F32)
            pskv = ps_kv.tile([P, BANK], F32)
            for c, acc in enumerate((psq, pskv)):
                nc.tensor.matmul_mx(
                    out=acc[:],
                    lhsT=hc[:, cols].bitcast(FP8X4),
                    lhsT_scale=hs[:, cols],
                    rhs=wc[:, BANK * c : BANK * c + BANK].bitcast(FP8X4),
                    rhs_scale=ws[:, BANK * c : BANK * c + BANK],
                    start=True,
                    stop=True,
                )
            st[("ps", i)] = (psq, pskv)

        def head_cols(i, h):
            psq, pskv = st[("ps", i)]
            if h < NQ:
                return psq[:, HD * h : HD * h + HD]
            return pskv[:, HD * (h - NQ) : HD * (h - NQ) + HD]

        def stage_headnorm(i, pair):
            u = i % 2
            if u == 0:
                o_t = o_pool.tile([P, 2, F], F32)
                st[("o", i // 2)] = o_t
            o_t = st[("o", i // 2)]
            if pair is None:
                ssh = small.tile([P, NH], F32)
                width = NH
            else:
                ssh = st[("sums", pair)]
                width = NH + 2
            junk_h = j_pool.tile([P, NH, HD], BF16)
            for h in range(NH):
                nc.scalar.activation(
                    out=junk_h[:, h, :], in_=head_cols(i, h), func=ACT.Square, scale=HD ** -0.5, accum_out=ssh[:, h : h + 1]
                )
            nc.scalar.copy(out=o_t[:, u, QK:F], in_=st[("ps", i)][1][:, BANK - (F - QK) : BANK])
            if i >= NT - SINGLE:
                ap, b, u = tile_coords(i)
                nc.sync.dma_start(out=o2v[b, :, 2 * ap + u : 2 * ap + u + 1, :], in_=o_t[:, u : u + 1, QK:F])
            rh = both_pool.tile([P, NH + 2], F32)
            nc.scalar.activation(
                out=rh[:, 0:width], in_=ssh[:, 0:width], func=ACT.Abs_reciprocal_sqrt, bias=eps_t[:]
            )
            if pair is not None:
                st[("rx", pair)] = rh[:, NH : NH + 1]
                st[("rx", pair + 1)] = rh[:, NH + 1 : NH + 2]
            st[("rh", i)] = rh

        def stage_rotate(i, h0, h1):
            ap, b, u = tile_coords(i)
            rh = st[("rh", i)]
            if h0 == 0:
                t_t = t_pool.tile([P, NH, 2 * HD], F32)
                st[("t", i)] = t_t
            t_t = st[("t", i)]
            for h in HEAD_ORDER[h0:h1]:
                nc.vector.scalar_tensor_tensor(
                    out=t_t[:, h, :].rearrange("p (d e) -> p d e", e=2),
                    in0=head_cols(i, h).unsqueeze(2).to_broadcast([P, HD, 2]),
                    scalar=rh[:, h : h + 1],
                    in1=tab[:, 2 * ap + u, 0 if h < NQ else 1, :, :].rearrange("p e d -> p d e"),
                    op0=ALU.mult,
                    op1=ALU.mult,
                )

        def sum_heads(i, h0, h1, eng):
            u = i % 2
            t_t = st[("t", i)]
            o_t = st[("o", i // 2)]
            eng.tensor_tensor(
                out=o_t[:, u, HD * h0 : HD * h1].rearrange("p (h d) -> p h d", d=HD),
                in0=t_t[:, h0:h1, 0:HD],
                in1=t_t[:, h0:h1, HD : 2 * HD],
                op=ALU.add,
            )

        def stage_sum(i):
            ap, b, u = tile_coords(i)
            o_t = st[("o", i // 2)]
            if i == NT - 2:
                sum_heads(i, 0, NQ, nc.gpsimd)
            else:
                sum_heads(i, 0, NH, nc.gpsimd)
            if i >= NT - SINGLE:
                us, sl = slice(u, u + 1), slice(2 * ap + u, 2 * ap + u + 1)
            elif u == 1:
                us, sl = slice(0, 2), slice(2 * ap, 2 * ap + 2)
            else:
                return
            nc.sync.dma_start(out=o0v[b, :, sl, :], in_=o_t[:, us, 0 : NQ * HD])
            if i != NT - 2:
                nc.sync.dma_start(out=o1v[b, :, sl, :], in_=o_t[:, us, NQ * HD : QK])
            if i < NT - SINGLE:
                nc.sync.dma_start(out=o2v[b, :, sl, :], in_=o_t[:, us, QK:F])

        def last_tile():
            i = NT - 1
            ap, b, u = tile_coords(i)
            o_t = st[("o", i // 2)]
            sl = slice(2 * ap + u, 2 * ap + u + 1)

            def add_and_store(h0):
                sum_heads(i, h0, h0 + 2, nc.vector)
                if h0 < NQ:
                    nc.sync.dma_start(out=o0v[b, :, sl, HD * h0 : HD * (h0 + 2)], in_=o_t[:, u : u + 1, HD * h0 : HD * (h0 + 2)])
                else:
                    nc.sync.dma_start(out=o1v[b, :, sl, :], in_=o_t[:, u : u + 1, NQ * HD : QK])

            stage_rotate(i, 0, 2)
            stage_rotate(i, 2, 4)
            sum_heads(i - 1, NQ, NH, nc.vector)
            nc.sync.dma_start(out=o1v[b, :, 2 * ap : 2 * ap + 1, :], in_=o_t[:, 0:1, NQ * HD : QK])
            add_and_store(HEAD_ORDER[0])
            stage_rotate(i, 4, 6)
            add_and_store(HEAD_ORDER[2])
            add_and_store(HEAD_ORDER[4])

        def on(stage, i):
            if 0 <= i < NT:
                stage(i)

        stage_square(0)
        stage_square(1)
        reduce_angles(0, FIRST_ANGLES)
        sines(0, FIRST_ANGLES)
        reduce_angles(FIRST_ANGLES, A)
        spread_rows()
        sines(FIRST_ANGLES, A)
        for i in range(0, EARLY, 2):
            early_rsqrt(i, 2)
        pieces = [(blk, piece) for blk in range(A // TABLE_BLOCK) for piece in range(3)]
        vector_pieces = pieces[: 3 * VECTOR_TABLES]
        weights()
        gate = const.tile([P, 1], U32)
        nc.gpsimd.tensor_copy(out=gate[:], in_=wc[:, F - 1 : F])
        for ap, piece in pieces[3 * VECTOR_TABLES : 3 * TABLES_AT_START]:
            table_piece(ap, piece, nc.gpsimd)
        later_pieces = pieces[3 * TABLES_AT_START :]

        for blk, piece in vector_pieces[:1]:
            table_piece(blk, piece, nc.vector)
        slots = NT + LAG_QUANT + 1
        written = 0
        pending = []
        for step in range(NT + LAG_SUM + 1):
            due = range(written, min(slots, slots_by_step(step)))
            written = max(written, min(slots, slots_by_step(step)))
            on(stage_matmul, step - LAG_MATMUL)
            if step - LAG_SUM < NT - 1:
                if step - LAG_SUM < VSUM:
                    on(stage_sum, step - LAG_SUM)
            if step >= PIECE_FROM and (step - PIECE_FROM) % PIECE_EVERY == 0 and later_pieces:
                table_piece(*later_pieces.pop(0), nc.gpsimd)
            merged = None
            if len(due) == 1 and due[0] % 2 == 0 and due[0] - LAG_RSQRT < NT and 0 <= step - LAG_HEADNORM < NT:
                merged = due[0] - LAG_RSQRT
            if 0 <= step - LAG_HEADNORM < NT:
                stage_headnorm(step - LAG_HEADNORM, merged)
            if step - LAG_ROTATE == NT - 1:
                last_tile()
            if 0 <= step - LAG_ROTATE < NT - 1:
                stage_rotate(step - LAG_ROTATE, 0, QUANT_AFTER)
            for qb, nb in pending:
                stage_quantise(qb, nb)
            pending = []
            if 0 <= step - LAG_ROTATE < NT - 1:
                stage_rotate(step - LAG_ROTATE, QUANT_AFTER, NH)
            for s in due:
                if s >= EARLY:
                    on(stage_square, s)
                if s - LAG_RSQRT >= EARLY and s % 2 == 0 and merged is None:
                    on(stage_rsqrt, s - LAG_RSQRT)
                on(stage_scale, s - LAG_SCALE)
                if s % 2 == 1:
                    on(stage_transpose, s - LAG_TRANSPOSE)
                else:
                    on(stage_round, s - LAG_ROUND)
            for s in due:
                i = s - LAG_QUANT
                if 0 <= i < NT and i == batches[i][1] + batches[i][2] - 1:
                    if step < LAG_ROTATE:
                        stage_quantise(batches[i][0], batches[i][2])
                    else:
                        pending.append((batches[i][0], batches[i][2]))
            if step == 0:
                for blk, piece in vector_pieces[1:]:
                    table_piece(blk, piece, nc.vector)
